import numpy as np
import ml_dtypes


def mxq(x, axis, fmt="e4m3"):
    dtype, down = {"e4m3": (ml_dtypes.float8_e4m3fn, 7), "e5m2": (ml_dtypes.float8_e5m2, 14)}[fmt]
    v = np.moveaxis(np.asarray(x, np.float32).astype(ml_dtypes.bfloat16).astype(np.float64), axis, -1)
    blocks = v.reshape(v.shape[:-1] + (-1, 32))
    amax = np.abs(blocks).max(-1, keepdims=True)
    byte = np.maximum(np.where(amax > 0, np.frexp(amax)[1] - 1 + 127, 0) - down, 1)
    scale = np.exp2(byte - 127.0)
    codes = (blocks / scale).astype(np.float32).astype(dtype).astype(np.float64)
    return np.moveaxis((codes * scale).reshape(v.shape), -1, axis)


BF16 = ml_dtypes.bfloat16


def bf(x):
    return np.asarray(x, np.float32).astype(BF16)


def f64(x):
    return np.asarray(x).astype(np.float64)


LQ, LK, D, H, DK, DV = 1024, 1024, 2048, 4, 128, 128
SQK = np.sqrt(2.0 * np.sqrt(D / DK))
SV = 3.0 * np.sqrt(LQ / LK)


def setup_inputs():
    return {"qh": bf(np.random.standard_normal((H, LQ, DK)) * SQK),
            "kh": bf(np.random.standard_normal((H, LK, DK)) * SQK),
            "vh": bf(np.random.standard_normal((H, LK, DV)) * SV)}


def reference(qh, kh, vh):
    scores = f64(qh) @ f64(kh).transpose(0, 2, 1) / np.sqrt(D)
    e = np.exp(scores - scores.max(axis=1, keepdims=True))
    attn = e / e.sum(axis=1, keepdims=True)
    return mxq(attn, 2, "e4m3") @ mxq(f64(vh), 1, "e4m3")

@@ -1,0 +1,254 @@
+from contextlib import ExitStack
+import math
+
+import concourse.mybir as mybir
+from concourse.masks import make_identity
+
+BF16 = mybir.dt.bfloat16
+F32 = mybir.dt.float32
+U32 = mybir.dt.uint32
+U8 = mybir.dt.uint8
+FP8X4 = mybir.dt.float8_e4m3fn_x4
+EXP = mybir.ActivationFunctionType.Exp
+ALU = mybir.AluOpType
+AXIS_X = mybir.AxisListType.X
+
+P = 128
+PACK = 4
+K_PASS = P * PACK
+HEADS, LQ, LK, DK, DV = 4, 1024, 1024, 128, 128
+PASSES = LK // K_PASS
+GROUPS = HEADS * PASSES
+Q_TILES = LQ // P
+BANK = 512
+HALVES = LQ // BANK
+SCORE_SCALE = 1.0 / math.sqrt(2048.0)
+SCALAR_QUERIES = 384
+
+FLOPS = 2 * HEADS * LQ * LK * (DK + DV)
+
+
+def tile_multiheadattention_pa_kernel(tc, qh, kh, vh, out):
+    nc = tc.nc
+    with ExitStack() as ctx:
+        const = ctx.enter_context(tc.tile_pool(name="const", bufs=1))
+        turned = ctx.enter_context(tc.tile_pool(name="turned", bufs=2))
+        stats = ctx.enter_context(tc.tile_pool(name="stats", bufs=6))
+        group_stats = ctx.enter_context(tc.tile_pool(name="group_stats", bufs=3))
+        e_pool = ctx.enter_context(tc.tile_pool(name="e_pool", bufs=3))
+        plane_pool = ctx.enter_context(tc.tile_pool(name="plane_pool", bufs=2))
+        grouped_pool = ctx.enter_context(tc.tile_pool(name="grouped_pool", bufs=2))
+        mx_pool = ctx.enter_context(tc.tile_pool(name="mx_pool", bufs=2))
+        out_pool = ctx.enter_context(tc.tile_pool(name="out_pool", bufs=3))
+        score_psum = ctx.enter_context(tc.psum_pool(name="score_psum", bufs=6))
+        aux_psum = ctx.enter_context(tc.psum_pool(name="aux_psum", bufs=2))
+        ctx.enter_context(tc.manual_schedule())
+
+        q_in = const.tile([P, HEADS, Q_TILES, DK], BF16)
+        k_in = const.tile([P, HEADS, PASSES, PACK, DK], BF16)
+        v_in = const.tile([P, HEADS * PASSES, PACK, DV], BF16)
+
+        def load_head(h):
+            nc.sync.dma_start(
+                out=k_in[:, h], in_=kh[h].rearrange("(g p j) d -> p g j d", g=PASSES, j=PACK)
+            )
+            nc.sync.dma_start(out=q_in[:, h], in_=qh[h].rearrange("(p t) d -> p t d", t=Q_TILES))
+
+        load_head(0)
+        nc.sync.dma_start(
+            out=v_in[:], in_=vh.rearrange("h (g p j) d -> p (h g) j d", g=PASSES, j=PACK)
+        )
+        for h in range(1, HEADS):
+            load_head(h)
+
+        ident = const.tile([P, P], BF16)
+        make_identity(nc, ident[:])
+
+        warm_in = const.tile([P, 1], F32)
+        warm_out = const.tile([P, 1], F32)
+        nc.vector.memset(warm_in[:], 0.0)
+        nc.scalar.activation(out=warm_out[:], in_=warm_in[:], func=EXP)
+
+        v_grouped = const.tile([P, HEADS * PASSES, DV, PACK], BF16, align_bytes=64)
+        v_words = const.tile([P, HEADS * PASSES, DV], U32, align_bytes=64)
+        v_scales = const.tile([P, HEADS * PASSES, DV], U8, align_bytes=64)
+
+        def regroup_values(h):
+            rows = slice(h * PASSES, (h + 1) * PASSES)
+            nc.gpsimd.tensor_scalar(
+                out=v_grouped[:, rows],
+                in0=v_in[:, rows].rearrange("p g j d -> p g d j"),
+                scalar1=1.0,
+                scalar2=0.0,
+                op0=ALU.mult,
+                op1=ALU.add,
+            )
+
+        def quantise_values():
+            nc.vector.quantize_mx(
+                out=v_words[:].rearrange("p g d -> p (g d)").bitcast(FP8X4),
+                scales=v_scales[:].rearrange("p g d -> p (g d)"),
+                in_=v_grouped[:].rearrange("p g d j -> p (g d j)"),
+            )
+
+        kT = {}
+        qT = {}
+
+        def transpose_keys(h):
+            bank = aux_psum.tile([P, PASSES * PACK, P], BF16, tag="aux", name="kT_ps%d" % h)
+            for g in range(PASSES):
+                for j in range(PACK):
+                    nc.tensor.transpose(bank[:, g * PACK + j, :], k_in[:, h, g, j, :], ident[:])
+            kT[h] = turned.tile([P, PASSES * PACK, P], BF16, tag="kT", name="kT%d" % h)
+            nc.vector.tensor_copy(out=kT[h][:], in_=bank[:])
+
+        def transpose_queries(h):
+            bank = aux_psum.tile([P, Q_TILES, P], BF16, tag="aux", name="qT_ps%d" % h)
+            for t in range(Q_TILES):
+                nc.tensor.transpose(bank[:, t, :], q_in[:, h, t, :], ident[:])
+            qT[h] = turned.tile([P, Q_TILES * P], BF16, tag="qT", name="qT%d" % h)
+            nc.scalar.copy(out=qT[h][:].rearrange("d (t p) -> d t p", p=P), in_=bank[:])
+
+        e_of = {}
+        sums_of = {}
+        recip_of = {}
+        planes_of = {}
+        grouped_of = {}
+        words_of = {}
+        scales_of = {}
+
+        def numerators(n, j):
+            h, g = divmod(n, PASSES)
+            if j == 0:
+                e_of[n] = e_pool.tile([P, PACK, LQ], F32, tag="e", name="e%d" % n)
+                sums_of[n] = group_stats.tile([P, PACK, HALVES], F32, tag="sums", name="sums%d" % n)
+            half_max = stats.tile([P, HALVES], F32, tag="half_max", name="half_max%d_%d" % (n, j))
+            shift = stats.tile([P, 1], F32, tag="shift", name="shift%d_%d" % (n, j))
+            banks = []
+            for c in range(HALVES):
+                bank = score_psum.tile([P, BANK], F32, tag="s", name="s%d_%d_%d" % (n, j, c))
+                banks.append(bank)
+                nc.tensor.matmul(
+                    bank[:],
+                    lhsT=kT[h][:, g * PACK + j, :],
+                    rhs=qT[h][:, c * BANK : (c + 1) * BANK],
+                    start=True,
+                    stop=True,
+                )
+                nc.vector.tensor_reduce(
+                    out=half_max[:, c : c + 1], in_=bank[:], axis=AXIS_X, op=ALU.max
+                )
+            nc.vector.tensor_scalar(
+                out=shift[:],
+                in0=half_max[:, 0:1],
+                scalar1=half_max[:, 1:2],
+                scalar2=-SCORE_SCALE,
+                op0=ALU.max,
+                op1=ALU.mult,
+            )
+            for c in range(HALVES):
+                nc.scalar.activation(
+                    out=e_of[n][:, j, c * BANK : (c + 1) * BANK],
+                    in_=banks[c][:],
+                    func=EXP,
+                    bias=shift[:, 0:1],
+                    scale=SCORE_SCALE,
+                    accum_out=sums_of[n][:, j, c : c + 1],
+                )
+
+        def normalise(n):
+            total = group_stats.tile([P, PACK], F32, tag="total", name="total%d" % n)
+            recip_of[n] = group_stats.tile([P, PACK], F32, tag="recip", name="recip%d" % n)
+            nc.vector.tensor_reduce(out=total[:], in_=sums_of[n][:], axis=AXIS_X, op=ALU.add)
+            nc.vector.reciprocal(out=recip_of[n][:], in_=total[:])
+            planes_of[n] = plane_pool.tile([P, PACK, LQ], BF16, tag="planes", name="planes%d" % n)
+            for j in range(PACK):
+                nc.gpsimd.tensor_scalar(
+                    out=planes_of[n][:, j, :],
+                    in0=e_of[n][:, j, :],
+                    scalar1=recip_of[n][:, j : j + 1],
+                    scalar2=0.0,
+                    op0=ALU.mult,
+                    op1=ALU.add,
+                )
+
+        def regroup(n):
+            grouped_of[n] = grouped_pool.tile(
+                [P, LQ, PACK], BF16, tag="grouped", name="grouped%d" % n, align_bytes=64
+            )
+            dst = grouped_of[n]
+            src = planes_of[n]
+            s = SCALAR_QUERIES
+            nc.scalar.copy(
+                out=dst[:, :s, :].rearrange("p (c i) j -> p c j i", i=4),
+                in_=src[:, :, :s].rearrange("p j (c i) -> p c j i", i=4),
+            )
+            nc.vector.tensor_copy(
+                out=dst[:, s:, :].rearrange("p (c i) j -> p c j i", i=4),
+                in_=src[:, :, s:].rearrange("p j (c i) -> p c j i", i=4),
+            )
+
+        def quantise(n):
+            h, g = divmod(n, PASSES)
+            if g == 0:
+                words_of[h] = mx_pool.tile(
+                    [P, PASSES, LQ], U32, tag="words", name="words%d" % h, align_bytes=64
+                )
+                scales_of[h] = mx_pool.tile(
+                    [P, PASSES, LQ], U8, tag="scales", name="scales%d" % h, align_bytes=64
+                )
+            nc.vector.quantize_mx(
+                out=words_of[h][:, g, :].bitcast(FP8X4),
+                scales=scales_of[h][:, g, :],
+                in_=grouped_of[n][:].rearrange("p q j -> p (q j)"),
+            )
+
+        def multiply(h):
+            rows = out[h].rearrange("(p t) d -> p t d", t=Q_TILES)
+            per_bank = BANK // DV
+            for b in range(Q_TILES // per_bank):
+                acc = aux_psum.tile([P, per_bank, DV], F32, tag="aux", name="acc%d_%d" % (h, b))
+                for i in range(per_bank):
+                    cols = slice((b * per_bank + i) * P, (b * per_bank + i + 1) * P)
+                    for g in range(PASSES):
+                        nc.tensor.matmul_mx(
+                            out=acc[:, i, :],
+                            lhsT=words_of[h][:, g, cols].bitcast(FP8X4),
+                            lhsT_scale=scales_of[h][:, g, cols],
+                            rhs=v_words[:, h * PASSES + g, :].bitcast(FP8X4),
+                            rhs_scale=v_scales[:, h * PASSES + g, :],
+                            start=(g == 0),
+                            stop=(g == PASSES - 1),
+                        )
+                result = out_pool.tile([P, per_bank, DV], F32, tag="result", name="res%d_%d" % (h, b))
+                if b % 2 == 0:
+                    nc.scalar.copy(out=result[:], in_=acc[:])
+                else:
+                    nc.vector.tensor_copy(out=result[:], in_=acc[:])
+                nc.sync.dma_start(out=rows[:, b * per_bank : (b + 1) * per_bank, :], in_=result[:])
+
+        transpose_keys(0)
+        transpose_queries(0)
+        for h in range(HEADS):
+            regroup_values(h)
+
+        for step in range(GROUPS + 4):
+            for j in range(PACK):
+                if step < GROUPS:
+                    numerators(step, j)
+                next_head = step // PASSES + 1
+                if step % PASSES == 0 and next_head < HEADS:
+                    if j == 0:
+                        transpose_keys(next_head)
+                    if j == 2:
+                        transpose_queries(next_head)
+                if step == 1 and j == 0:
+                    quantise_values()
+                if j == 2 and 0 <= step - 1 < GROUPS:
+                    normalise(step - 1)
+                if j == 3 and 0 <= step - 2 < GROUPS:
+                    regroup(step - 2)
+                if j == 1 and 0 <= step - 3 < GROUPS:
+                    quantise(step - 3)
+                if j == 3 and 0 <= step - 3 < GROUPS and (step - 3) % PASSES == PASSES - 1:
+                    multiply((step - 3) // PASSES)

@@ -23,7 +23,8 @@ Q_TILES = LQ // P
 BANK = 512
 HALVES = LQ // BANK
 SCORE_SCALE = 1.0 / math.sqrt(2048.0)
-SCALAR_QUERIES = 384
+PAIR = 2
+SCALAR_QUERIES = 224
 
 FLOPS = 2 * HEADS * LQ * LK * (DK + DV)
 
@@ -34,32 +35,37 @@ def tile_multiheadattention_pa_kernel(tc, qh, kh, vh, out):
         const = ctx.enter_context(tc.tile_pool(name="const", bufs=1))
         turned = ctx.enter_context(tc.tile_pool(name="turned", bufs=2))
         stats = ctx.enter_context(tc.tile_pool(name="stats", bufs=6))
-        group_stats = ctx.enter_context(tc.tile_pool(name="group_stats", bufs=3))
         e_pool = ctx.enter_context(tc.tile_pool(name="e_pool", bufs=3))
         plane_pool = ctx.enter_context(tc.tile_pool(name="plane_pool", bufs=2))
         grouped_pool = ctx.enter_context(tc.tile_pool(name="grouped_pool", bufs=2))
         mx_pool = ctx.enter_context(tc.tile_pool(name="mx_pool", bufs=2))
         out_pool = ctx.enter_context(tc.tile_pool(name="out_pool", bufs=3))
-        score_psum = ctx.enter_context(tc.psum_pool(name="score_psum", bufs=6))
-        aux_psum = ctx.enter_context(tc.psum_pool(name="aux_psum", bufs=2))
+        psum = ctx.enter_context(tc.psum_pool(name="psum", bufs=8))
         ctx.enter_context(tc.manual_schedule())
 
         q_in = const.tile([P, HEADS, Q_TILES, DK], BF16)
-        k_in = const.tile([P, HEADS, PASSES, PACK, DK], BF16)
+        k_in = const.tile([P, HEADS, PASSES * PACK, DK], BF16)
         v_in = const.tile([P, HEADS * PASSES, PACK, DV], BF16)
 
-        def load_head(h):
+        def load_keys(h, g):
             nc.sync.dma_start(
-                out=k_in[:, h], in_=kh[h].rearrange("(g p j) d -> p g j d", g=PASSES, j=PACK)
+                out=k_in[:, h, g * PACK : (g + 1) * PACK, :],
+                in_=kh[h, g * K_PASS : (g + 1) * K_PASS, :].rearrange("(p j) d -> p j d", j=PACK),
             )
+
+        def load_queries(h):
             nc.sync.dma_start(out=q_in[:, h], in_=qh[h].rearrange("(p t) d -> p t d", t=Q_TILES))
 
-        load_head(0)
+        load_keys(0, 0)
+        load_queries(0)
+        load_keys(0, 1)
         nc.sync.dma_start(
             out=v_in[:], in_=vh.rearrange("h (g p j) d -> p (h g) j d", g=PASSES, j=PACK)
         )
         for h in range(1, HEADS):
-            load_head(h)
+            load_keys(h, 0)
+            load_queries(h)
+            load_keys(h, 1)
 
         ident = const.tile([P, P], BF16)
         make_identity(nc, ident[:])
@@ -94,54 +100,61 @@ def tile_multiheadattention_pa_kernel(tc, qh, kh, vh, out):
         kT = {}
         qT = {}
 
-        def transpose_keys(h):
-            bank = aux_psum.tile([P, PASSES * PACK, P], BF16, tag="aux", name="kT_ps%d" % h)
-            for g in range(PASSES):
-                for j in range(PACK):
-                    nc.tensor.transpose(bank[:, g * PACK + j, :], k_in[:, h, g, j, :], ident[:])
-            kT[h] = turned.tile([P, PASSES * PACK, P], BF16, tag="kT", name="kT%d" % h)
-            nc.vector.tensor_copy(out=kT[h][:], in_=bank[:])
-
-        def transpose_queries(h):
-            bank = aux_psum.tile([P, Q_TILES, P], BF16, tag="aux", name="qT_ps%d" % h)
-            for t in range(Q_TILES):
-                nc.tensor.transpose(bank[:, t, :], q_in[:, h, t, :], ident[:])
-            qT[h] = turned.tile([P, Q_TILES * P], BF16, tag="qT", name="qT%d" % h)
-            nc.scalar.copy(out=qT[h][:].rearrange("d (t p) -> d t p", p=P), in_=bank[:])
+        def transpose_part(h, part):
+            if part == 0:
+                kT[h] = turned.tile([P, PASSES * PACK * P], BF16, tag="kT", name="kT%d" % h)
+                qT[h] = turned.tile([P, LQ], BF16, tag="qT", name="qT%d" % h)
+            keys = part in (0, 3)
+            source, target = (k_in, kT[h]) if keys else (q_in, qT[h])
+            half = part // 2 if keys else part - 1
+            bank = psum.tile([P, BANK], BF16, tag="bank", name="turn%d_%d" % (h, part))
+            for i in range(PACK):
+                nc.tensor.transpose(
+                    bank[:, i * P : (i + 1) * P], source[:, h, half * PACK + i, :], ident[:]
+                )
+            if part % 2 == 0:
+                nc.vector.tensor_copy(out=target[:, half * BANK : (half + 1) * BANK], in_=bank[:])
+            else:
+                nc.scalar.copy(out=target[:, half * BANK : (half + 1) * BANK], in_=bank[:])
 
         e_of = {}
         sums_of = {}
-        recip_of = {}
         planes_of = {}
         grouped_of = {}
         words_of = {}
         scales_of = {}
+        banks_of = {}
+        half_max_of = {}
+        total_of = {}
 
-        def numerators(n, j):
+        def score_maxima(n, j):
             h, g = divmod(n, PASSES)
-            if j == 0:
-                e_of[n] = e_pool.tile([P, PACK, LQ], F32, tag="e", name="e%d" % n)
-                sums_of[n] = group_stats.tile([P, PACK, HALVES], F32, tag="sums", name="sums%d" % n)
-            half_max = stats.tile([P, HALVES], F32, tag="half_max", name="half_max%d_%d" % (n, j))
-            shift = stats.tile([P, 1], F32, tag="shift", name="shift%d_%d" % (n, j))
-            banks = []
+            half_max_of[n, j] = stats.tile([P, HALVES], F32, tag="half_max", name="half_max%d_%d" % (n, j))
+            banks_of[n, j] = []
+            tile_cols = slice((g * PACK + j) * P, (g * PACK + j + 1) * P)
             for c in range(HALVES):
-                bank = score_psum.tile([P, BANK], F32, tag="s", name="s%d_%d_%d" % (n, j, c))
-                banks.append(bank)
+                bank = psum.tile([P, BANK], F32, tag="bank", name="s%d_%d_%d" % (n, j, c))
+                banks_of[n, j].append(bank)
                 nc.tensor.matmul(
                     bank[:],
-                    lhsT=kT[h][:, g * PACK + j, :],
+                    lhsT=kT[h][:, tile_cols],
                     rhs=qT[h][:, c * BANK : (c + 1) * BANK],
                     start=True,
                     stop=True,
                 )
                 nc.vector.tensor_reduce(
-                    out=half_max[:, c : c + 1], in_=bank[:], axis=AXIS_X, op=ALU.max
+                    out=half_max_of[n, j][:, c : c + 1], in_=bank[:], axis=AXIS_X, op=ALU.max
                 )
+
+        def exponentials(n, j):
+            if j == 0:
+                e_of[n] = e_pool.tile([P, PACK, LQ], F32, tag="e", name="e%d" % n)
+                sums_of[n] = stats.tile([P, PACK, HALVES], F32, tag="sums", name="sums%d" % n)
+            shift = stats.tile([P, 1], F32, tag="shift", name="shift%d_%d" % (n, j))
             nc.vector.tensor_scalar(
                 out=shift[:],
-                in0=half_max[:, 0:1],
-                scalar1=half_max[:, 1:2],
+                in0=half_max_of[n, j][:, 0:1],
+                scalar1=half_max_of[n, j][:, 1:2],
                 scalar2=-SCORE_SCALE,
                 op0=ALU.max,
                 op1=ALU.mult,
@@ -149,65 +162,78 @@ def tile_multiheadattention_pa_kernel(tc, qh, kh, vh, out):
             for c in range(HALVES):
                 nc.scalar.activation(
                     out=e_of[n][:, j, c * BANK : (c + 1) * BANK],
-                    in_=banks[c][:],
+                    in_=banks_of[n, j][c][:],
                     func=EXP,
                     bias=shift[:, 0:1],
                     scale=SCORE_SCALE,
                     accum_out=sums_of[n][:, j, c : c + 1],
                 )
 
-        def normalise(n):
-            total = group_stats.tile([P, PACK], F32, tag="total", name="total%d" % n)
-            recip_of[n] = group_stats.tile([P, PACK], F32, tag="recip", name="recip%d" % n)
-            nc.vector.tensor_reduce(out=total[:], in_=sums_of[n][:], axis=AXIS_X, op=ALU.add)
-            nc.vector.reciprocal(out=recip_of[n][:], in_=total[:])
-            planes_of[n] = plane_pool.tile([P, PACK, LQ], BF16, tag="planes", name="planes%d" % n)
-            for j in range(PACK):
-                nc.gpsimd.tensor_scalar(
+        def add_halves(n, pair):
+            total_of[n, pair] = stats.tile([P, PAIR], F32, tag="total", name="total%d_%d" % (n, pair))
+            nc.vector.tensor_reduce(
+                out=total_of[n, pair][:],
+                in_=sums_of[n][:, pair * PAIR : (pair + 1) * PAIR, :],
+                axis=AXIS_X,
+                op=ALU.add,
+            )
+
+        def normalise(n, pair):
+            recip = stats.tile([P, PAIR], F32, tag="recip", name="recip%d_%d" % (n, pair))
+            nc.vector.reciprocal(out=recip[:], in_=total_of[n, pair][:])
+            if pair == 0:
+                planes_of[n] = plane_pool.tile([P, PACK, LQ], BF16, tag="planes", name="planes%d" % n)
+            for i in range(PAIR):
+                j = pair * PAIR + i
+                last = n == GROUPS - 1 and j == PACK - 1
+                engine = nc.vector if last else nc.gpsimd
+                engine.tensor_scalar(
                     out=planes_of[n][:, j, :],
                     in0=e_of[n][:, j, :],
-                    scalar1=recip_of[n][:, j : j + 1],
+                    scalar1=recip[:, i : i + 1],
                     scalar2=0.0,
                     op0=ALU.mult,
                     op1=ALU.add,
                 )
 
-        def regroup(n):
-            grouped_of[n] = grouped_pool.tile(
-                [P, LQ, PACK], BF16, tag="grouped", name="grouped%d" % n, align_bytes=64
-            )
+        def regroup(n, c):
+            if c == 0:
+                grouped_of[n] = grouped_pool.tile(
+                    [P, LQ, PACK], BF16, tag="grouped", name="grouped%d" % n, align_bytes=64
+                )
             dst = grouped_of[n]
             src = planes_of[n]
-            s = SCALAR_QUERIES
+            lo, mid, hi = c * BANK, c * BANK + SCALAR_QUERIES, (c + 1) * BANK
             nc.scalar.copy(
-                out=dst[:, :s, :].rearrange("p (c i) j -> p c j i", i=4),
-                in_=src[:, :, :s].rearrange("p j (c i) -> p c j i", i=4),
+                out=dst[:, lo:mid, :].rearrange("p (c i) j -> p c j i", i=4),
+                in_=src[:, :, lo:mid].rearrange("p j (c i) -> p c j i", i=4),
             )
             nc.vector.tensor_copy(
-                out=dst[:, s:, :].rearrange("p (c i) j -> p c j i", i=4),
-                in_=src[:, :, s:].rearrange("p j (c i) -> p c j i", i=4),
+                out=dst[:, mid:hi, :].rearrange("p (c i) j -> p c j i", i=4),
+                in_=src[:, :, mid:hi].rearrange("p j (c i) -> p c j i", i=4),
             )
 
-        def quantise(n):
+        def quantise(n, c):
             h, g = divmod(n, PASSES)
-            if g == 0:
+            if g == 0 and c == 0:
                 words_of[h] = mx_pool.tile(
                     [P, PASSES, LQ], U32, tag="words", name="words%d" % h, align_bytes=64
                 )
                 scales_of[h] = mx_pool.tile(
                     [P, PASSES, LQ], U8, tag="scales", name="scales%d" % h, align_bytes=64
                 )
+            cols = slice(c * BANK, (c + 1) * BANK)
             nc.vector.quantize_mx(
-                out=words_of[h][:, g, :].bitcast(FP8X4),
-                scales=scales_of[h][:, g, :],
-                in_=grouped_of[n][:].rearrange("p q j -> p (q j)"),
+                out=words_of[h][:, g, cols].bitcast(FP8X4),
+                scales=scales_of[h][:, g, cols],
+                in_=grouped_of[n][:, cols, :].rearrange("p q j -> p (q j)"),
             )
 
         def multiply(h):
             rows = out[h].rearrange("(p t) d -> p t d", t=Q_TILES)
             per_bank = BANK // DV
             for b in range(Q_TILES // per_bank):
-                acc = aux_psum.tile([P, per_bank, DV], F32, tag="aux", name="acc%d_%d" % (h, b))
+                acc = psum.tile([P, per_bank, DV], F32, tag="bank", name="acc%d_%d" % (h, b))
                 for i in range(per_bank):
                     cols = slice((b * per_bank + i) * P, (b * per_bank + i + 1) * P)
                     for g in range(PASSES):
@@ -227,28 +253,32 @@ def tile_multiheadattention_pa_kernel(tc, qh, kh, vh, out):
                     nc.vector.tensor_copy(out=result[:], in_=acc[:])
                 nc.sync.dma_start(out=rows[:, b * per_bank : (b + 1) * per_bank, :], in_=result[:])
 
-        transpose_keys(0)
-        transpose_queries(0)
+        for part in range(4):
+            transpose_part(0, part)
         for h in range(HEADS):
             regroup_values(h)
 
         for step in range(GROUPS + 4):
             for j in range(PACK):
+                pair_group = step if j == 3 else step - 1
+                pair = 0 if j == 3 else 1
+                pair_due = j % 2 == 1 and 0 <= pair_group < GROUPS
                 if step < GROUPS:
-                    numerators(step, j)
-                next_head = step // PASSES + 1
-                if step % PASSES == 0 and next_head < HEADS:
-                    if j == 0:
-                        transpose_keys(next_head)
-                    if j == 2:
-                        transpose_queries(next_head)
+                    score_maxima(step, j)
+                if pair_due:
+                    add_halves(pair_group, pair)
+                if 0 <= step - 2 < GROUPS:
+                    if j < HALVES:
+                        regroup(step - 2, j)
+                    else:
+                        quantise(step - 2, j - HALVES)
                 if step == 1 and j == 0:
                     quantise_values()
-                if j == 2 and 0 <= step - 1 < GROUPS:
-                    normalise(step - 1)
-                if j == 3 and 0 <= step - 2 < GROUPS:
-                    regroup(step - 2)
-                if j == 1 and 0 <= step - 3 < GROUPS:
-                    quantise(step - 3)
-                if j == 3 and 0 <= step - 3 < GROUPS and (step - 3) % PASSES == PASSES - 1:
-                    multiply((step - 3) // PASSES)
+                if step < GROUPS:
+                    exponentials(step, j)
+                if pair_due:
+                    normalise(pair_group, pair)
+                if step % PASSES == 0 and step // PASSES + 1 < HEADS:
+                    transpose_part(step // PASSES + 1, j)
+                if step % PASSES == 1 and step >= 5 and j == 0:
+                    multiply((step - 5) // PASSES)

@@ -24,7 +24,7 @@ BANK = 512
 HALVES = LQ // BANK
 SCORE_SCALE = 1.0 / math.sqrt(2048.0)
 PAIR = 2
-SCALAR_QUERIES = 224
+SCALAR_QUERIES = 256
 
 FLOPS = 2 * HEADS * LQ * LK * (DK + DV)
 
@@ -56,16 +56,14 @@ def tile_multiheadattention_pa_kernel(tc, qh, kh, vh, out):
         def load_queries(h):
             nc.sync.dma_start(out=q_in[:, h], in_=qh[h].rearrange("(p t) d -> p t d", t=Q_TILES))
 
-        load_keys(0, 0)
-        load_queries(0)
-        load_keys(0, 1)
-        nc.sync.dma_start(
-            out=v_in[:], in_=vh.rearrange("h (g p j) d -> p (h g) j d", g=PASSES, j=PACK)
-        )
-        for h in range(1, HEADS):
+        for h in range(HEADS):
             load_keys(h, 0)
             load_queries(h)
             load_keys(h, 1)
+            if h == 1:
+                nc.sync.dma_start(
+                    out=v_in[:], in_=vh.rearrange("h (g p j) d -> p (h g) j d", g=PASSES, j=PACK)
+                )
 
         ident = const.tile([P, P], BF16)
         make_identity(nc, ident[:])
@@ -112,7 +110,7 @@ def tile_multiheadattention_pa_kernel(tc, qh, kh, vh, out):
                 nc.tensor.transpose(
                     bank[:, i * P : (i + 1) * P], source[:, h, half * PACK + i, :], ident[:]
                 )
-            if part % 2 == 0:
+            if h == 0 and part % 2 == 0:
                 nc.vector.tensor_copy(out=target[:, half * BANK : (half + 1) * BANK], in_=bank[:])
             else:
                 nc.scalar.copy(out=target[:, half * BANK : (half + 1) * BANK], in_=bank[:])
@@ -247,10 +245,10 @@ def tile_multiheadattention_pa_kernel(tc, qh, kh, vh, out):
                             stop=(g == PASSES - 1),
                         )
                 result = out_pool.tile([P, per_bank, DV], F32, tag="result", name="res%d_%d" % (h, b))
-                if b % 2 == 0:
-                    nc.scalar.copy(out=result[:], in_=acc[:])
-                else:
+                if h == HEADS - 1 and b == 1:
                     nc.vector.tensor_copy(out=result[:], in_=acc[:])
+                else:
+                    nc.scalar.copy(out=result[:], in_=acc[:])
                 nc.sync.dma_start(out=rows[:, b * per_bank : (b + 1) * per_bank, :], in_=result[:])
 
         for part in range(4):

@@ -10,6 +10,7 @@ U32 = mybir.dt.uint32
 U8 = mybir.dt.uint8
 FP8X4 = mybir.dt.float8_e4m3fn_x4
 EXP = mybir.ActivationFunctionType.Exp
+COPY = mybir.ActivationFunctionType.Copy
 ALU = mybir.AluOpType
 AXIS_X = mybir.AxisListType.X
 
@@ -23,8 +24,11 @@ Q_TILES = LQ // P
 BANK = 512
 HALVES = LQ // BANK
 SCORE_SCALE = 1.0 / math.sqrt(2048.0)
-PAIR = 2
-SCALAR_QUERIES = 256
+RUN = 4
+
+STEADY = (BANK, 128, 64)
+LAST = (256, 128, 64)
+GPSIMD_QUERIES = 64
 
 FLOPS = 2 * HEADS * LQ * LK * (DK + DV)
 
@@ -36,11 +40,11 @@ def tile_multiheadattention_pa_kernel(tc, qh, kh, vh, out):
         turned = ctx.enter_context(tc.tile_pool(name="turned", bufs=2))
         stats = ctx.enter_context(tc.tile_pool(name="stats", bufs=6))
         e_pool = ctx.enter_context(tc.tile_pool(name="e_pool", bufs=3))
-        plane_pool = ctx.enter_context(tc.tile_pool(name="plane_pool", bufs=2))
-        grouped_pool = ctx.enter_context(tc.tile_pool(name="grouped_pool", bufs=2))
+        plane_pool = ctx.enter_context(tc.tile_pool(name="plane_pool", bufs=3))
+        grouped_pool = ctx.enter_context(tc.tile_pool(name="grouped_pool", bufs=3))
         mx_pool = ctx.enter_context(tc.tile_pool(name="mx_pool", bufs=2))
-        out_pool = ctx.enter_context(tc.tile_pool(name="out_pool", bufs=3))
-        psum = ctx.enter_context(tc.psum_pool(name="psum", bufs=8))
+        out_pool = ctx.enter_context(tc.tile_pool(name="out_pool", bufs=4))
+        psum = ctx.enter_context(tc.psum_pool(name="psum", bufs=7))
         ctx.enter_context(tc.manual_schedule())
 
         q_in = const.tile([P, HEADS, Q_TILES, DK], BF16)
@@ -53,12 +57,17 @@ def tile_multiheadattention_pa_kernel(tc, qh, kh, vh, out):
                 in_=kh[h, g * K_PASS : (g + 1) * K_PASS, :].rearrange("(p j) d -> p j d", j=PACK),
             )
 
-        def load_queries(h):
-            nc.sync.dma_start(out=q_in[:, h], in_=qh[h].rearrange("(p t) d -> p t d", t=Q_TILES))
+        def load_queries(h, t0, t1):
+            rows = qh[h].rearrange("(p t) d -> p t d", t=Q_TILES)
+            nc.sync.dma_start(out=q_in[:, h, t0:t1], in_=rows[:, t0:t1, :])
 
         for h in range(HEADS):
             load_keys(h, 0)
-            load_queries(h)
+            if h == 0:
+                load_queries(h, 0, PACK)
+                load_queries(h, PACK, Q_TILES)
+            else:
+                load_queries(h, 0, Q_TILES)
             load_keys(h, 1)
             if h == 1:
                 nc.sync.dma_start(
@@ -67,6 +76,8 @@ def tile_multiheadattention_pa_kernel(tc, qh, kh, vh, out):
 
         ident = const.tile([P, P], BF16)
         make_identity(nc, ident[:])
+        ident_f32 = const.tile([P, P], F32)
+        make_identity(nc, ident_f32[:])
 
         warm_in = const.tile([P, 1], F32)
         warm_out = const.tile([P, 1], F32)
@@ -117,13 +128,15 @@ def tile_multiheadattention_pa_kernel(tc, qh, kh, vh, out):
 
         e_of = {}
         sums_of = {}
-        planes_of = {}
+        total_of = {}
+        recip_of = {}
+        spread_of = {}
         grouped_of = {}
         words_of = {}
         scales_of = {}
         banks_of = {}
         half_max_of = {}
-        total_of = {}
+        shift_of = {}
 
         def score_maxima(n, j):
             h, g = divmod(n, PASSES)
@@ -144,11 +157,8 @@ def tile_multiheadattention_pa_kernel(tc, qh, kh, vh, out):
                     out=half_max_of[n, j][:, c : c + 1], in_=bank[:], axis=AXIS_X, op=ALU.max
                 )
 
-        def exponentials(n, j):
-            if j == 0:
-                e_of[n] = e_pool.tile([P, PACK, LQ], F32, tag="e", name="e%d" % n)
-                sums_of[n] = stats.tile([P, PACK, HALVES], F32, tag="sums", name="sums%d" % n)
-            shift = stats.tile([P, 1], F32, tag="shift", name="shift%d_%d" % (n, j))
+        def exponentials_shift(n, j):
+            shift = shift_of[n, j] = stats.tile([P, 1], F32, tag="shift", name="shift%d_%d" % (n, j))
             nc.vector.tensor_scalar(
                 out=shift[:],
                 in0=half_max_of[n, j][:, 0:1],
@@ -157,126 +167,180 @@ def tile_multiheadattention_pa_kernel(tc, qh, kh, vh, out):
                 op0=ALU.max,
                 op1=ALU.mult,
             )
+
+        def exponentials(n, j):
+            if j == 0:
+                e_of[n] = e_pool.tile([P, PACK, LQ], F32, tag="e", name="e%d" % n)
+                sums_of[n] = stats.tile([P, PACK, HALVES], F32, tag="sums", name="sums%d" % n)
             for c in range(HALVES):
                 nc.scalar.activation(
                     out=e_of[n][:, j, c * BANK : (c + 1) * BANK],
                     in_=banks_of[n, j][c][:],
                     func=EXP,
-                    bias=shift[:, 0:1],
+                    bias=shift_of[n, j][:, 0:1],
                     scale=SCORE_SCALE,
                     accum_out=sums_of[n][:, j, c : c + 1],
                 )
 
-        def add_halves(n, pair):
-            total_of[n, pair] = stats.tile([P, PAIR], F32, tag="total", name="total%d_%d" % (n, pair))
-            nc.vector.tensor_reduce(
-                out=total_of[n, pair][:],
-                in_=sums_of[n][:, pair * PAIR : (pair + 1) * PAIR, :],
-                axis=AXIS_X,
-                op=ALU.add,
+        def add_halves(n):
+            total_of[n] = stats.tile([P, PACK], F32, tag="total", name="total%d" % n)
+            nc.vector.tensor_reduce(out=total_of[n][:], in_=sums_of[n][:], axis=AXIS_X, op=ALU.add)
+
+        def invert(n):
+            recip_of[n] = stats.tile([P, PACK], F32, tag="recip", name="recip%d" % n)
+            nc.vector.reciprocal(out=recip_of[n][:], in_=total_of[n][:])
+            grouped_of[n] = grouped_pool.tile(
+                [P, LQ, PACK], BF16, tag="grouped", name="grouped%d" % n, align_bytes=64
             )
 
-        def normalise(n, pair):
-            recip = stats.tile([P, PAIR], F32, tag="recip", name="recip%d_%d" % (n, pair))
-            nc.vector.reciprocal(out=recip[:], in_=total_of[n, pair][:])
-            if pair == 0:
-                planes_of[n] = plane_pool.tile([P, PACK, LQ], BF16, tag="planes", name="planes%d" % n)
-            for i in range(PAIR):
-                j = pair * PAIR + i
-                last = n == GROUPS - 1 and j == PACK - 1
-                engine = nc.vector if last else nc.gpsimd
-                engine.tensor_scalar(
-                    out=planes_of[n][:, j, :],
-                    in0=e_of[n][:, j, :],
-                    scalar1=recip[:, i : i + 1],
-                    scalar2=0.0,
-                    op0=ALU.mult,
-                    op1=ALU.add,
-                )
+        def spread(n):
+            spread_of[n] = psum.tile([P, PACK], F32, tag="spread", name="spread%d" % n, bufs=1)
+            nc.tensor.matmul(
+                spread_of[n][:], lhsT=ident_f32[:], rhs=recip_of[n][:], start=True, stop=True
+            )
 
-        def regroup(n, c):
-            if c == 0:
-                grouped_of[n] = grouped_pool.tile(
-                    [P, LQ, PACK], BF16, tag="grouped", name="grouped%d" % n, align_bytes=64
+        def spans(n):
+            span, by_vector, by_scalar = LAST if n == GROUPS - 1 else STEADY
+            return [(lo, span, by_vector, by_scalar) for lo in range(0, LQ, span)]
+
+        def multiply_and_group(engine, n, factors, lo, hi):
+            runs = (hi - lo) // RUN
+            engine.tensor_tensor(
+                out=grouped_of[n][:, lo:hi, :].rearrange("p (c i) j -> p c j i", i=RUN),
+                in0=e_of[n][:, :, lo:hi].rearrange("p j (c i) -> p c j i", i=RUN),
+                in1=factors[:].unsqueeze(1).unsqueeze(3).to_broadcast([P, runs, PACK, RUN]),
+                op=ALU.mult,
+            )
+
+        def group_by_vector(n, k):
+            lo, span, by_vector, by_scalar = spans(n)[k]
+            multiply_and_group(nc.vector, n, spread_of[n], lo, lo + by_vector)
+
+        def group_by_gpsimd(n, k):
+            lo, span, by_vector, by_scalar = spans(n)[k]
+            for q in range(lo + by_vector + by_scalar, lo + span, GPSIMD_QUERIES):
+                multiply_and_group(nc.gpsimd, n, recip_of[n], q, q + GPSIMD_QUERIES)
+
+        def group_by_scalar(n, k):
+            lo, span, by_vector, by_scalar = spans(n)[k]
+            first, end = lo + by_vector, lo + by_vector + by_scalar
+            planes = plane_pool.tile([P, PACK, by_scalar], BF16, tag="planes", name="planes%d_%d" % (n, k))
+            for j in range(PACK):
+                nc.scalar.activation(
+                    out=planes[:, j, :],
+                    in_=e_of[n][:, j, first:end],
+                    func=COPY,
+                    scale=recip_of[n][:, j : j + 1],
                 )
-            dst = grouped_of[n]
-            src = planes_of[n]
-            lo, mid, hi = c * BANK, c * BANK + SCALAR_QUERIES, (c + 1) * BANK
             nc.scalar.copy(
-                out=dst[:, lo:mid, :].rearrange("p (c i) j -> p c j i", i=4),
-                in_=src[:, :, lo:mid].rearrange("p j (c i) -> p c j i", i=4),
-            )
-            nc.vector.tensor_copy(
-                out=dst[:, mid:hi, :].rearrange("p (c i) j -> p c j i", i=4),
-                in_=src[:, :, mid:hi].rearrange("p j (c i) -> p c j i", i=4),
+                out=grouped_of[n][:, first:end, :].rearrange("p (c i) j -> p c j i", i=RUN),
+                in_=planes[:].rearrange("p j (c i) -> p c j i", i=RUN),
             )
 
-        def quantise(n, c):
+        def quantise(n, k):
             h, g = divmod(n, PASSES)
-            if g == 0 and c == 0:
+            if g == 0 and k == 0:
                 words_of[h] = mx_pool.tile(
                     [P, PASSES, LQ], U32, tag="words", name="words%d" % h, align_bytes=64
                 )
                 scales_of[h] = mx_pool.tile(
                     [P, PASSES, LQ], U8, tag="scales", name="scales%d" % h, align_bytes=64
                 )
-            cols = slice(c * BANK, (c + 1) * BANK)
+            lo, span, by_vector, by_scalar = spans(n)[k]
+            cols = slice(lo, lo + span)
             nc.vector.quantize_mx(
                 out=words_of[h][:, g, cols].bitcast(FP8X4),
                 scales=scales_of[h][:, g, cols],
                 in_=grouped_of[n][:, cols, :].rearrange("p q j -> p (q j)"),
             )
 
-        def multiply(h):
+        def multiply(h, t0, t1, engine):
             rows = out[h].rearrange("(p t) d -> p t d", t=Q_TILES)
-            per_bank = BANK // DV
-            for b in range(Q_TILES // per_bank):
-                acc = psum.tile([P, per_bank, DV], F32, tag="bank", name="acc%d_%d" % (h, b))
-                for i in range(per_bank):
-                    cols = slice((b * per_bank + i) * P, (b * per_bank + i + 1) * P)
-                    for g in range(PASSES):
-                        nc.tensor.matmul_mx(
-                            out=acc[:, i, :],
-                            lhsT=words_of[h][:, g, cols].bitcast(FP8X4),
-                            lhsT_scale=scales_of[h][:, g, cols],
-                            rhs=v_words[:, h * PASSES + g, :].bitcast(FP8X4),
-                            rhs_scale=v_scales[:, h * PASSES + g, :],
-                            start=(g == 0),
-                            stop=(g == PASSES - 1),
-                        )
-                result = out_pool.tile([P, per_bank, DV], F32, tag="result", name="res%d_%d" % (h, b))
-                if h == HEADS - 1 and b == 1:
-                    nc.vector.tensor_copy(out=result[:], in_=acc[:])
-                else:
-                    nc.scalar.copy(out=result[:], in_=acc[:])
-                nc.sync.dma_start(out=rows[:, b * per_bank : (b + 1) * per_bank, :], in_=result[:])
+            acc = psum.tile([P, t1 - t0, DV], F32, tag="bank", name="acc%d_%d" % (h, t0))
+            for t in range(t0, t1):
+                cols = slice(t * P, (t + 1) * P)
+                for g in range(PASSES):
+                    nc.tensor.matmul_mx(
+                        out=acc[:, t - t0, :],
+                        lhsT=words_of[h][:, g, cols].bitcast(FP8X4),
+                        lhsT_scale=scales_of[h][:, g, cols],
+                        rhs=v_words[:, h * PASSES + g, :].bitcast(FP8X4),
+                        rhs_scale=v_scales[:, h * PASSES + g, :],
+                        start=(g == 0),
+                        stop=(g == PASSES - 1),
+                    )
+            result = out_pool.tile([P, t1 - t0, DV], F32, tag="result", name="res%d_%d" % (h, t0))
+            if engine == "vector":
+                nc.vector.tensor_copy(out=result[:], in_=acc[:])
+            else:
+                nc.scalar.copy(out=result[:], in_=acc[:])
+            nc.sync.dma_start(out=rows[:, t0:t1, :], in_=result[:])
 
         for part in range(4):
             transpose_part(0, part)
         for h in range(HEADS):
             regroup_values(h)
 
-        for step in range(GROUPS + 4):
-            for j in range(PACK):
-                pair_group = step if j == 3 else step - 1
-                pair = 0 if j == 3 else 1
-                pair_due = j % 2 == 1 and 0 <= pair_group < GROUPS
-                if step < GROUPS:
-                    score_maxima(step, j)
-                if pair_due:
-                    add_halves(pair_group, pair)
-                if 0 <= step - 2 < GROUPS:
-                    if j < HALVES:
-                        regroup(step - 2, j)
-                    else:
-                        quantise(step - 2, j - HALVES)
-                if step == 1 and j == 0:
-                    quantise_values()
-                if step < GROUPS:
-                    exponentials(step, j)
-                if pair_due:
-                    normalise(pair_group, pair)
-                if step % PASSES == 0 and step // PASSES + 1 < HEADS:
-                    transpose_part(step // PASSES + 1, j)
-                if step % PASSES == 1 and step >= 5 and j == 0:
-                    multiply((step - 5) // PASSES)
+        last = GROUPS - 1
+        for slot in range(GROUPS * PACK):
+            n, j = divmod(slot, PACK)
+
+            def due(lag):
+                m, rest = divmod(slot - lag, PACK)
+                return m if rest == 0 and 0 <= m < last else None
+
+            score_maxima(n, j)
+            if due(5) is not None:
+                spread(due(5))
+            if due(4) is not None:
+                add_halves(due(4))
+            if due(5) is not None:
+                group_by_vector(due(5), 0)
+            if due(6) is not None:
+                group_by_vector(due(6), 1)
+            exponentials_shift(n, j)
+            if due(4) is not None:
+                invert(due(4))
+                for k in range(len(spans(due(4)))):
+                    group_by_gpsimd(due(4), k)
+            if due(8) is not None:
+                quantise(due(8), 0)
+            if due(10) is not None:
+                quantise(due(10), 1)
+            if slot == 7:
+                quantise_values()
+            exponentials(n, j)
+            if due(5) is not None:
+                group_by_scalar(due(5), 0)
+            if due(7) is not None:
+                group_by_scalar(due(7), 1)
+            if n % PASSES == 0 and n // PASSES + 1 < HEADS:
+                transpose_part(n // PASSES + 1, j)
+            for b, lag in ((0, 9), (1, 11)):
+                m = due(lag)
+                if m is not None and m % PASSES == PASSES - 1:
+                    multiply(m // PASSES, b * PACK, (b + 1) * PACK, "scalar")
+
+        quantise(last - 1, 0)
+        add_halves(last)
+        invert(last)
+        spread(last)
+        for k in range(len(spans(last))):
+            group_by_gpsimd(last, k)
+        group_by_scalar(last, 0)
+        quantise(last - 1, 1)
+        group_by_vector(last, 0)
+        group_by_vector(last, 1)
+        group_by_scalar(last, 1)
+        quantise(last, 0)
+        group_by_vector(last, 2)
+        group_by_scalar(last, 2)
+        multiply(HEADS - 1, 0, 2, "scalar")
+        quantise(last, 1)
+        group_by_vector(last, 3)
+        group_by_scalar(last, 3)
+        multiply(HEADS - 1, 2, 4, "scalar")
+        quantise(last, 2)
+        multiply(HEADS - 1, 4, 6, "scalar")
+        quantise(last, 3)
+        multiply(HEADS - 1, 6, 8, "vector")

@@ -28,7 +28,6 @@ RUN = 4
 
 STEADY = (BANK, 128, 64)
 LAST = (256, 128, 64)
-GPSIMD_QUERIES = 64
 
 FLOPS = 2 * HEADS * LQ * LK * (DK + DV)
 
@@ -41,7 +40,7 @@ def tile_multiheadattention_pa_kernel(tc, qh, kh, vh, out):
         stats = ctx.enter_context(tc.tile_pool(name="stats", bufs=6))
         e_pool = ctx.enter_context(tc.tile_pool(name="e_pool", bufs=3))
         plane_pool = ctx.enter_context(tc.tile_pool(name="plane_pool", bufs=3))
-        grouped_pool = ctx.enter_context(tc.tile_pool(name="grouped_pool", bufs=3))
+        grouped_pool = ctx.enter_context(tc.tile_pool(name="grouped_pool", bufs=2))
         mx_pool = ctx.enter_context(tc.tile_pool(name="mx_pool", bufs=2))
         out_pool = ctx.enter_context(tc.tile_pool(name="out_pool", bufs=4))
         psum = ctx.enter_context(tc.psum_pool(name="psum", bufs=7))
@@ -189,15 +188,21 @@ def tile_multiheadattention_pa_kernel(tc, qh, kh, vh, out):
         def invert(n):
             recip_of[n] = stats.tile([P, PACK], F32, tag="recip", name="recip%d" % n)
             nc.vector.reciprocal(out=recip_of[n][:], in_=total_of[n][:])
-            grouped_of[n] = grouped_pool.tile(
-                [P, LQ, PACK], BF16, tag="grouped", name="grouped%d" % n, align_bytes=64
-            )
 
         def spread(n):
             spread_of[n] = psum.tile([P, PACK], F32, tag="spread", name="spread%d" % n, bufs=1)
             nc.tensor.matmul(
                 spread_of[n][:], lhsT=ident_f32[:], rhs=recip_of[n][:], start=True, stop=True
             )
+
+        def open_half(n, c):
+            grouped_of[n, c] = grouped_pool.tile(
+                [P, BANK, PACK], BF16, tag="grouped", name="grouped%d_%d" % (n, c), align_bytes=64
+            )
+
+        def grouped(n, lo, hi):
+            c = lo // BANK
+            return grouped_of[n, c][:, lo - c * BANK : hi - c * BANK, :]
 
         def spans(n):
             span, by_vector, by_scalar = LAST if n == GROUPS - 1 else STEADY
@@ -206,7 +211,7 @@ def tile_multiheadattention_pa_kernel(tc, qh, kh, vh, out):
         def multiply_and_group(engine, n, factors, lo, hi):
             runs = (hi - lo) // RUN
             engine.tensor_tensor(
-                out=grouped_of[n][:, lo:hi, :].rearrange("p (c i) j -> p c j i", i=RUN),
+                out=grouped(n, lo, hi).rearrange("p (c i) j -> p c j i", i=RUN),
                 in0=e_of[n][:, :, lo:hi].rearrange("p j (c i) -> p c j i", i=RUN),
                 in1=factors[:].unsqueeze(1).unsqueeze(3).to_broadcast([P, runs, PACK, RUN]),
                 op=ALU.mult,
@@ -218,8 +223,7 @@ def tile_multiheadattention_pa_kernel(tc, qh, kh, vh, out):
 
         def group_by_gpsimd(n, k):
             lo, span, by_vector, by_scalar = spans(n)[k]
-            for q in range(lo + by_vector + by_scalar, lo + span, GPSIMD_QUERIES):
-                multiply_and_group(nc.gpsimd, n, recip_of[n], q, q + GPSIMD_QUERIES)
+            multiply_and_group(nc.gpsimd, n, recip_of[n], lo + by_vector + by_scalar, lo + span)
 
         def group_by_scalar(n, k):
             lo, span, by_vector, by_scalar = spans(n)[k]
@@ -233,7 +237,7 @@ def tile_multiheadattention_pa_kernel(tc, qh, kh, vh, out):
                     scale=recip_of[n][:, j : j + 1],
                 )
             nc.scalar.copy(
-                out=grouped_of[n][:, first:end, :].rearrange("p (c i) j -> p c j i", i=RUN),
+                out=grouped(n, first, end).rearrange("p (c i) j -> p c j i", i=RUN),
                 in_=planes[:].rearrange("p j (c i) -> p c j i", i=RUN),
             )
 
@@ -251,7 +255,7 @@ def tile_multiheadattention_pa_kernel(tc, qh, kh, vh, out):
             nc.vector.quantize_mx(
                 out=words_of[h][:, g, cols].bitcast(FP8X4),
                 scales=scales_of[h][:, g, cols],
-                in_=grouped_of[n][:, cols, :].rearrange("p q j -> p (q j)"),
+                in_=grouped(n, lo, lo + span).rearrange("p q j -> p (q j)"),
             )
 
         def multiply(h, t0, t1, engine):
@@ -296,17 +300,18 @@ def tile_multiheadattention_pa_kernel(tc, qh, kh, vh, out):
                 add_halves(due(4))
             if due(5) is not None:
                 group_by_vector(due(5), 0)
-            if due(6) is not None:
-                group_by_vector(due(6), 1)
+            if due(7) is not None:
+                group_by_vector(due(7), 1)
             exponentials_shift(n, j)
             if due(4) is not None:
                 invert(due(4))
-                for k in range(len(spans(due(4)))):
-                    group_by_gpsimd(due(4), k)
-            if due(8) is not None:
-                quantise(due(8), 0)
-            if due(10) is not None:
-                quantise(due(10), 1)
+            for k, lag in ((0, 8), (1, 10)):
+                if due(lag) is not None:
+                    quantise(due(lag), k)
+            for k, lag in ((0, 4), (1, 6)):
+                if due(lag) is not None:
+                    open_half(due(lag), k)
+                    group_by_gpsimd(due(lag), k)
             if slot == 7:
                 quantise_values()
             exponentials(n, j)
@@ -325,11 +330,15 @@ def tile_multiheadattention_pa_kernel(tc, qh, kh, vh, out):
         add_halves(last)
         invert(last)
         spread(last)
-        for k in range(len(spans(last))):
-            group_by_gpsimd(last, k)
+        open_half(last, 0)
+        group_by_gpsimd(last, 0)
+        group_by_gpsimd(last, 1)
+        group_by_vector(last, 0)
         group_by_scalar(last, 0)
         quantise(last - 1, 1)
-        group_by_vector(last, 0)
+        open_half(last, 1)
+        group_by_gpsimd(last, 2)
+        group_by_gpsimd(last, 3)
         group_by_vector(last, 1)
         group_by_scalar(last, 1)
         quantise(last, 0)

@@ -26,8 +26,12 @@ HALVES = LQ // BANK
 SCORE_SCALE = 1.0 / math.sqrt(2048.0)
 RUN = 4
 
-STEADY = (BANK, 128, 64)
-LAST = (256, 128, 64)
+VECTOR_QUERIES, VECTOR_PARTS, SCALAR_QUERIES = 288, 3, 96
+QUARTER = LQ // 4
+JOIN = 5
+LATE = 192
+SLAG = 5
+TURNS = ((0, 1), (2, 3), (), ())
 
 FLOPS = 2 * HEADS * LQ * LK * (DK + DV)
 
@@ -40,7 +44,7 @@ def tile_multiheadattention_pa_kernel(tc, qh, kh, vh, out):
         stats = ctx.enter_context(tc.tile_pool(name="stats", bufs=6))
         e_pool = ctx.enter_context(tc.tile_pool(name="e_pool", bufs=3))
         plane_pool = ctx.enter_context(tc.tile_pool(name="plane_pool", bufs=3))
-        grouped_pool = ctx.enter_context(tc.tile_pool(name="grouped_pool", bufs=2))
+        grouped_pool = ctx.enter_context(tc.tile_pool(name="grouped_pool", bufs=1))
         mx_pool = ctx.enter_context(tc.tile_pool(name="mx_pool", bufs=2))
         out_pool = ctx.enter_context(tc.tile_pool(name="out_pool", bufs=4))
         psum = ctx.enter_context(tc.psum_pool(name="psum", bufs=7))
@@ -195,67 +199,53 @@ def tile_multiheadattention_pa_kernel(tc, qh, kh, vh, out):
                 spread_of[n][:], lhsT=ident_f32[:], rhs=recip_of[n][:], start=True, stop=True
             )
 
-        def open_half(n, c):
-            grouped_of[n, c] = grouped_pool.tile(
-                [P, BANK, PACK], BF16, tag="grouped", name="grouped%d_%d" % (n, c), align_bytes=64
+        def open_group(n):
+            grouped_of[n] = grouped_pool.tile(
+                [P, LQ, PACK], BF16, tag="grouped", name="grouped%d" % n, align_bytes=64
             )
-
-        def grouped(n, lo, hi):
-            c = lo // BANK
-            return grouped_of[n, c][:, lo - c * BANK : hi - c * BANK, :]
-
-        def spans(n):
-            span, by_vector, by_scalar = LAST if n == GROUPS - 1 else STEADY
-            return [(lo, span, by_vector, by_scalar) for lo in range(0, LQ, span)]
 
         def multiply_and_group(engine, n, factors, lo, hi):
             runs = (hi - lo) // RUN
             engine.tensor_tensor(
-                out=grouped(n, lo, hi).rearrange("p (c i) j -> p c j i", i=RUN),
+                out=grouped_of[n][:, lo:hi, :].rearrange("p (c i) j -> p c j i", i=RUN),
                 in0=e_of[n][:, :, lo:hi].rearrange("p j (c i) -> p c j i", i=RUN),
                 in1=factors[:].unsqueeze(1).unsqueeze(3).to_broadcast([P, runs, PACK, RUN]),
                 op=ALU.mult,
             )
 
-        def group_by_vector(n, k):
-            lo, span, by_vector, by_scalar = spans(n)[k]
-            multiply_and_group(nc.vector, n, spread_of[n], lo, lo + by_vector)
+        def group_by_vector(n, lo, hi):
+            multiply_and_group(nc.vector, n, spread_of[n], lo, hi)
 
-        def group_by_gpsimd(n, k):
-            lo, span, by_vector, by_scalar = spans(n)[k]
-            multiply_and_group(nc.gpsimd, n, recip_of[n], lo + by_vector + by_scalar, lo + span)
+        def group_by_gpsimd(n, lo, hi):
+            multiply_and_group(nc.gpsimd, n, recip_of[n], lo, hi)
 
-        def group_by_scalar(n, k):
-            lo, span, by_vector, by_scalar = spans(n)[k]
-            first, end = lo + by_vector, lo + by_vector + by_scalar
-            planes = plane_pool.tile([P, PACK, by_scalar], BF16, tag="planes", name="planes%d_%d" % (n, k))
+        def group_by_scalar(n, lo, hi):
+            planes = plane_pool.tile([P, PACK, hi - lo], BF16, tag="planes%d" % (hi - lo), name="planes%d" % n)
             for j in range(PACK):
                 nc.scalar.activation(
                     out=planes[:, j, :],
-                    in_=e_of[n][:, j, first:end],
+                    in_=e_of[n][:, j, lo:hi],
                     func=COPY,
                     scale=recip_of[n][:, j : j + 1],
                 )
             nc.scalar.copy(
-                out=grouped(n, first, end).rearrange("p (c i) j -> p c j i", i=RUN),
+                out=grouped_of[n][:, lo:hi, :].rearrange("p (c i) j -> p c j i", i=RUN),
                 in_=planes[:].rearrange("p j (c i) -> p c j i", i=RUN),
             )
 
-        def quantise(n, k):
+        def quantise(n, lo, hi):
             h, g = divmod(n, PASSES)
-            if g == 0 and k == 0:
+            if g == 0 and lo == 0:
                 words_of[h] = mx_pool.tile(
                     [P, PASSES, LQ], U32, tag="words", name="words%d" % h, align_bytes=64
                 )
                 scales_of[h] = mx_pool.tile(
                     [P, PASSES, LQ], U8, tag="scales", name="scales%d" % h, align_bytes=64
                 )
-            lo, span, by_vector, by_scalar = spans(n)[k]
-            cols = slice(lo, lo + span)
             nc.vector.quantize_mx(
-                out=words_of[h][:, g, cols].bitcast(FP8X4),
-                scales=scales_of[h][:, g, cols],
-                in_=grouped(n, lo, lo + span).rearrange("p q j -> p (q j)"),
+                out=words_of[h][:, g, lo:hi].bitcast(FP8X4),
+                scales=scales_of[h][:, g, lo:hi],
+                in_=grouped_of[n][:, lo:hi, :].rearrange("p q j -> p (q j)"),
             )
 
         def multiply(h, t0, t1, engine):
@@ -294,62 +284,49 @@ def tile_multiheadattention_pa_kernel(tc, qh, kh, vh, out):
                 return m if rest == 0 and 0 <= m < last else None
 
             score_maxima(n, j)
-            if due(5) is not None:
-                spread(due(5))
-            if due(4) is not None:
-                add_halves(due(4))
-            if due(5) is not None:
-                group_by_vector(due(5), 0)
-            if due(7) is not None:
-                group_by_vector(due(7), 1)
+            if due(JOIN + 1) is not None:
+                spread(due(JOIN + 1))
+            if due(JOIN) is not None:
+                add_halves(due(JOIN))
+            for part in range(VECTOR_PARTS):
+                if due(JOIN + 1 + part) is not None:
+                    step = VECTOR_QUERIES // VECTOR_PARTS
+                    group_by_vector(due(JOIN + 1 + part), part * step, (part + 1) * step)
             exponentials_shift(n, j)
-            if due(4) is not None:
-                invert(due(4))
-            for k, lag in ((0, 8), (1, 10)):
-                if due(lag) is not None:
-                    quantise(due(lag), k)
-            for k, lag in ((0, 4), (1, 6)):
-                if due(lag) is not None:
-                    open_half(due(lag), k)
-                    group_by_gpsimd(due(lag), k)
-            if slot == 7:
+            if slot == JOIN:
                 quantise_values()
+            if due(JOIN) is not None:
+                invert(due(JOIN))
+            if due(JOIN + 4) is not None:
+                quantise(due(JOIN + 4), 0, LQ)
+            if due(JOIN) is not None:
+                open_group(due(JOIN))
+                first = VECTOR_QUERIES + SCALAR_QUERIES
+                group_by_gpsimd(due(JOIN), first + (LATE if due(JOIN) == last - 1 else 0), LQ)
             exponentials(n, j)
-            if due(5) is not None:
-                group_by_scalar(due(5), 0)
-            if due(7) is not None:
-                group_by_scalar(due(7), 1)
+            if due(SLAG) is not None:
+                group_by_scalar(due(SLAG), VECTOR_QUERIES, VECTOR_QUERIES + SCALAR_QUERIES)
             if n % PASSES == 0 and n // PASSES + 1 < HEADS:
-                transpose_part(n // PASSES + 1, j)
-            for b, lag in ((0, 9), (1, 11)):
+                for part in TURNS[j]:
+                    transpose_part(n // PASSES + 1, part)
+            for b, lag in ((0, JOIN + 5), (1, JOIN + 6)):
                 m = due(lag)
                 if m is not None and m % PASSES == PASSES - 1:
                     multiply(m // PASSES, b * PACK, (b + 1) * PACK, "scalar")
 
-        quantise(last - 1, 0)
+        if VECTOR_PARTS + JOIN == 8:
+            step = VECTOR_QUERIES // VECTOR_PARTS
+            group_by_vector(last - 1, VECTOR_QUERIES - step, VECTOR_QUERIES)
+        group_by_vector(last - 1, VECTOR_QUERIES + SCALAR_QUERIES, VECTOR_QUERIES + SCALAR_QUERIES + LATE)
         add_halves(last)
         invert(last)
         spread(last)
-        open_half(last, 0)
-        group_by_gpsimd(last, 0)
-        group_by_gpsimd(last, 1)
-        group_by_vector(last, 0)
-        group_by_scalar(last, 0)
-        quantise(last - 1, 1)
-        open_half(last, 1)
-        group_by_gpsimd(last, 2)
-        group_by_gpsimd(last, 3)
-        group_by_vector(last, 1)
-        group_by_scalar(last, 1)
-        quantise(last, 0)
-        group_by_vector(last, 2)
-        group_by_scalar(last, 2)
-        multiply(HEADS - 1, 0, 2, "scalar")
-        quantise(last, 1)
-        group_by_vector(last, 3)
-        group_by_scalar(last, 3)
-        multiply(HEADS - 1, 2, 4, "scalar")
-        quantise(last, 2)
-        multiply(HEADS - 1, 4, 6, "scalar")
-        quantise(last, 3)
-        multiply(HEADS - 1, 6, 8, "vector")
+        quantise(last - 1, 0, LQ)
+        open_group(last)
+        group_by_gpsimd(last, 2 * QUARTER, 3 * QUARTER)
+        group_by_scalar(last, 3 * QUARTER, LQ)
+        group_by_vector(last, 0, QUARTER)
+        group_by_vector(last, QUARTER, 2 * QUARTER)
+        for k in range(4):
+            quantise(last, k * QUARTER, (k + 1) * QUARTER)
+            multiply(HEADS - 1, 2 * k, 2 * k + 2, "vector" if k == 3 else "scalar")

@@ -26,12 +26,14 @@ HALVES = LQ // BANK
 SCORE_SCALE = 1.0 / math.sqrt(2048.0)
 RUN = 4
 
-VECTOR_QUERIES, VECTOR_PARTS, SCALAR_QUERIES = 288, 3, 96
-QUARTER = LQ // 4
+VECTOR_QUERIES, SCALAR_QUERIES = 264, 144
+VECTOR_PARTS = 3
+VECTOR_MORE = 192
+LAST_VECTOR, LAST_GPSIMD = 512, 192
+EARLY = 3
+TURN_GROUPS = (1, 2, 4)
 JOIN = 5
-LATE = 192
-SLAG = 5
-TURNS = ((0, 1), (2, 3), (), ())
+TURNS = ((0,), (1,), (2,), (3,))
 
 FLOPS = 2 * HEADS * LQ * LK * (DK + DV)
 
@@ -46,7 +48,7 @@ def tile_multiheadattention_pa_kernel(tc, qh, kh, vh, out):
         plane_pool = ctx.enter_context(tc.tile_pool(name="plane_pool", bufs=3))
         grouped_pool = ctx.enter_context(tc.tile_pool(name="grouped_pool", bufs=1))
         mx_pool = ctx.enter_context(tc.tile_pool(name="mx_pool", bufs=2))
-        out_pool = ctx.enter_context(tc.tile_pool(name="out_pool", bufs=4))
+        out_pool = ctx.enter_context(tc.tile_pool(name="out_pool", bufs=8))
         psum = ctx.enter_context(tc.psum_pool(name="psum", bufs=7))
         ctx.enter_context(tc.manual_schedule())
 
@@ -72,7 +74,7 @@ def tile_multiheadattention_pa_kernel(tc, qh, kh, vh, out):
             else:
                 load_queries(h, 0, Q_TILES)
             load_keys(h, 1)
-            if h == 1:
+            if h == 0:
                 nc.sync.dma_start(
                     out=v_in[:], in_=vh.rearrange("h (g p j) d -> p (h g) j d", g=PASSES, j=PACK)
                 )
@@ -124,10 +126,14 @@ def tile_multiheadattention_pa_kernel(tc, qh, kh, vh, out):
                 nc.tensor.transpose(
                     bank[:, i * P : (i + 1) * P], source[:, h, half * PACK + i, :], ident[:]
                 )
-            if h == 0 and part % 2 == 0:
-                nc.vector.tensor_copy(out=target[:, half * BANK : (half + 1) * BANK], in_=bank[:])
+            lo, mid, hi = half * BANK, half * BANK + BANK // 2, (half + 1) * BANK
+            if h == 0 and part == 1:
+                nc.scalar.copy(out=target[:, lo:mid], in_=bank[:, : BANK // 2])
+                nc.vector.tensor_copy(out=target[:, mid:hi], in_=bank[:, BANK // 2 :])
+            elif h == 0 and part % 2 == 0:
+                nc.vector.tensor_copy(out=target[:, lo:hi], in_=bank[:])
             else:
-                nc.scalar.copy(out=target[:, half * BANK : (half + 1) * BANK], in_=bank[:])
+                nc.scalar.copy(out=target[:, lo:hi], in_=bank[:])
 
         e_of = {}
         sums_of = {}
@@ -141,7 +147,7 @@ def tile_multiheadattention_pa_kernel(tc, qh, kh, vh, out):
         half_max_of = {}
         shift_of = {}
 
-        def score_maxima(n, j):
+        def scores(n, j):
             h, g = divmod(n, PASSES)
             half_max_of[n, j] = stats.tile([P, HALVES], F32, tag="half_max", name="half_max%d_%d" % (n, j))
             banks_of[n, j] = []
@@ -156,14 +162,16 @@ def tile_multiheadattention_pa_kernel(tc, qh, kh, vh, out):
                     start=True,
                     stop=True,
                 )
-                nc.vector.tensor_reduce(
-                    out=half_max_of[n, j][:, c : c + 1], in_=bank[:], axis=AXIS_X, op=ALU.max
-                )
 
-        def exponentials_shift(n, j):
-            shift = shift_of[n, j] = stats.tile([P, 1], F32, tag="shift", name="shift%d_%d" % (n, j))
+        def maximum(n, j, c):
+            nc.vector.tensor_reduce(
+                out=half_max_of[n, j][:, c : c + 1], in_=banks_of[n, j][c][:], axis=AXIS_X, op=ALU.max
+            )
+
+        def shift(n, j):
+            shift_of[n, j] = stats.tile([P, 1], F32, tag="shift", name="shift%d_%d" % (n, j))
             nc.vector.tensor_scalar(
-                out=shift[:],
+                out=shift_of[n, j][:],
                 in0=half_max_of[n, j][:, 0:1],
                 scalar1=half_max_of[n, j][:, 1:2],
                 scalar2=-SCORE_SCALE,
@@ -276,6 +284,8 @@ def tile_multiheadattention_pa_kernel(tc, qh, kh, vh, out):
             regroup_values(h)
 
         last = GROUPS - 1
+        step = VECTOR_QUERIES // VECTOR_PARTS
+        scalar_end = VECTOR_QUERIES + SCALAR_QUERIES
         for slot in range(GROUPS * PACK):
             n, j = divmod(slot, PACK)
 
@@ -283,50 +293,58 @@ def tile_multiheadattention_pa_kernel(tc, qh, kh, vh, out):
                 m, rest = divmod(slot - lag, PACK)
                 return m if rest == 0 and 0 <= m < last else None
 
-            score_maxima(n, j)
+            scores(n, j)
+            joined, ready = due(JOIN), due(JOIN + 4)
+            maximum(n, j, 0)
+            if 0 < slot <= EARLY:
+                shift(*divmod(slot - 1, PACK))
+                exponentials(*divmod(slot - 1, PACK))
+            if joined is not None:
+                add_halves(joined)
+            maximum(n, j, 1)
             if due(JOIN + 1) is not None:
                 spread(due(JOIN + 1))
-            if due(JOIN) is not None:
-                add_halves(due(JOIN))
             for part in range(VECTOR_PARTS):
-                if due(JOIN + 1 + part) is not None:
-                    step = VECTOR_QUERIES // VECTOR_PARTS
-                    group_by_vector(due(JOIN + 1 + part), part * step, (part + 1) * step)
-            exponentials_shift(n, j)
+                m = due(JOIN + 1 + part)
+                if m is not None:
+                    group_by_vector(m, part * step, (part + 1) * step)
             if slot == JOIN:
+                shift(n, j)
                 quantise_values()
-            if due(JOIN) is not None:
-                invert(due(JOIN))
-            if due(JOIN + 4) is not None:
-                quantise(due(JOIN + 4), 0, LQ)
-            if due(JOIN) is not None:
-                open_group(due(JOIN))
-                first = VECTOR_QUERIES + SCALAR_QUERIES
-                group_by_gpsimd(due(JOIN), first + (LATE if due(JOIN) == last - 1 else 0), LQ)
-            exponentials(n, j)
-            if due(SLAG) is not None:
-                group_by_scalar(due(SLAG), VECTOR_QUERIES, VECTOR_QUERIES + SCALAR_QUERIES)
-            if n % PASSES == 0 and n // PASSES + 1 < HEADS:
+            if joined is not None:
+                invert(joined)
+            if slot >= EARLY and slot != JOIN:
+                shift(n, j)
+            if ready is not None:
+                quantise(ready, 0, LQ)
+            if joined is not None:
+                open_group(joined)
+                group_by_gpsimd(joined, scalar_end + (VECTOR_MORE if joined == last - 1 else 0), LQ)
+            if slot >= EARLY:
+                exponentials(n, j)
+            if joined is not None:
+                group_by_scalar(joined, VECTOR_QUERIES, scalar_end)
+            if n in TURN_GROUPS:
                 for part in TURNS[j]:
-                    transpose_part(n // PASSES + 1, part)
+                    transpose_part(1 + TURN_GROUPS.index(n), part)
             for b, lag in ((0, JOIN + 5), (1, JOIN + 6)):
                 m = due(lag)
-                if m is not None and m % PASSES == PASSES - 1:
+                if m is not None and m % PASSES == PASSES - 1 and n < last:
                     multiply(m // PASSES, b * PACK, (b + 1) * PACK, "scalar")
 
-        if VECTOR_PARTS + JOIN == 8:
-            step = VECTOR_QUERIES // VECTOR_PARTS
-            group_by_vector(last - 1, VECTOR_QUERIES - step, VECTOR_QUERIES)
-        group_by_vector(last - 1, VECTOR_QUERIES + SCALAR_QUERIES, VECTOR_QUERIES + SCALAR_QUERIES + LATE)
+        group_by_vector(last - 1, 2 * step, VECTOR_QUERIES)
+        group_by_vector(last - 1, scalar_end, scalar_end + VECTOR_MORE)
         add_halves(last)
         invert(last)
         spread(last)
         quantise(last - 1, 0, LQ)
         open_group(last)
-        group_by_gpsimd(last, 2 * QUARTER, 3 * QUARTER)
-        group_by_scalar(last, 3 * QUARTER, LQ)
-        group_by_vector(last, 0, QUARTER)
-        group_by_vector(last, QUARTER, 2 * QUARTER)
-        for k in range(4):
-            quantise(last, k * QUARTER, (k + 1) * QUARTER)
-            multiply(HEADS - 1, 2 * k, 2 * k + 2, "vector" if k == 3 else "scalar")
+        group_by_gpsimd(last, LAST_VECTOR, LAST_VECTOR + LAST_GPSIMD)
+        group_by_scalar(last, LAST_VECTOR + LAST_GPSIMD, LQ)
+        group_by_vector(last, 0, LAST_VECTOR // 2)
+        group_by_vector(last, LAST_VECTOR // 2, LAST_VECTOR)
+        for b in range(2):
+            multiply(HEADS - 2, b * PACK, (b + 1) * PACK, "scalar")
+        for t0, t1 in ((0, 2), (2, 4), (4, 6), (6, 7), (7, 8)):
+            quantise(last, t0 * P, t1 * P)
+            multiply(HEADS - 1, t0, t1, "vector" if t0 == 7 else "scalar")

@@ -26,11 +26,13 @@ HALVES = LQ // BANK
 SCORE_SCALE = 1.0 / math.sqrt(2048.0)
 RUN = 4
 
-VECTOR_QUERIES, SCALAR_QUERIES = 264, 144
-VECTOR_PARTS = 3
-VECTOR_MORE = 192
+VECTOR_QUERIES, SCALAR_QUERIES = 256, 144
+VECTOR_PARTS = 4
+VECTOR_MORE = 128
 LAST_VECTOR, LAST_GPSIMD = 512, 192
 EARLY = 3
+FIRST_VECTOR, FIRST_SCALAR = 352, 0
+QV2 = 9
 TURN_GROUPS = (1, 2, 4)
 JOIN = 5
 TURNS = ((0,), (1,), (2,), (3,))
@@ -75,9 +77,11 @@ def tile_multiheadattention_pa_kernel(tc, qh, kh, vh, out):
                 load_queries(h, 0, Q_TILES)
             load_keys(h, 1)
             if h == 0:
-                nc.sync.dma_start(
-                    out=v_in[:], in_=vh.rearrange("h (g p j) d -> p (h g) j d", g=PASSES, j=PACK)
-                )
+                for k in range(HEADS):
+                    nc.sync.dma_start(
+                        out=v_in[:, k * PASSES : (k + 1) * PASSES],
+                        in_=vh[k].rearrange("(g p j) d -> p g j d", g=PASSES, j=PACK),
+                    )
 
         ident = const.tile([P, P], BF16)
         make_identity(nc, ident[:])
@@ -104,11 +108,12 @@ def tile_multiheadattention_pa_kernel(tc, qh, kh, vh, out):
                 op1=ALU.add,
             )
 
-        def quantise_values():
+        def quantise_values(h0, h1):
+            rows = slice(h0 * PASSES, h1 * PASSES)
             nc.vector.quantize_mx(
-                out=v_words[:].rearrange("p g d -> p (g d)").bitcast(FP8X4),
-                scales=v_scales[:].rearrange("p g d -> p (g d)"),
-                in_=v_grouped[:].rearrange("p g d j -> p (g d j)"),
+                out=v_words[:, rows].rearrange("p g d -> p (g d)").bitcast(FP8X4),
+                scales=v_scales[:, rows].rearrange("p g d -> p (g d)"),
+                in_=v_grouped[:, rows].rearrange("p g d j -> p (g d j)"),
             )
 
         kT = {}
@@ -143,29 +148,29 @@ def tile_multiheadattention_pa_kernel(tc, qh, kh, vh, out):
         grouped_of = {}
         words_of = {}
         scales_of = {}
-        banks_of = {}
+        bank_of = {}
         half_max_of = {}
         shift_of = {}
 
-        def scores(n, j):
+        def scores(n, j, c):
             h, g = divmod(n, PASSES)
-            half_max_of[n, j] = stats.tile([P, HALVES], F32, tag="half_max", name="half_max%d_%d" % (n, j))
-            banks_of[n, j] = []
             tile_cols = slice((g * PACK + j) * P, (g * PACK + j + 1) * P)
-            for c in range(HALVES):
-                bank = psum.tile([P, BANK], F32, tag="bank", name="s%d_%d_%d" % (n, j, c))
-                banks_of[n, j].append(bank)
-                nc.tensor.matmul(
-                    bank[:],
-                    lhsT=kT[h][:, tile_cols],
-                    rhs=qT[h][:, c * BANK : (c + 1) * BANK],
-                    start=True,
-                    stop=True,
-                )
+            bank_of[n, j, c] = psum.tile([P, BANK], F32, tag="bank", name="s%d_%d_%d" % (n, j, c))
+            nc.tensor.matmul(
+                bank_of[n, j, c][:],
+                lhsT=kT[h][:, tile_cols],
+                rhs=qT[h][:, c * BANK : (c + 1) * BANK],
+                start=True,
+                stop=True,
+            )
 
         def maximum(n, j, c):
+            if c == 0:
+                half_max_of[n, j] = stats.tile(
+                    [P, HALVES], F32, tag="half_max", name="half_max%d_%d" % (n, j)
+                )
             nc.vector.tensor_reduce(
-                out=half_max_of[n, j][:, c : c + 1], in_=banks_of[n, j][c][:], axis=AXIS_X, op=ALU.max
+                out=half_max_of[n, j][:, c : c + 1], in_=bank_of[n, j, c][:], axis=AXIS_X, op=ALU.max
             )
 
         def shift(n, j):
@@ -186,7 +191,7 @@ def tile_multiheadattention_pa_kernel(tc, qh, kh, vh, out):
             for c in range(HALVES):
                 nc.scalar.activation(
                     out=e_of[n][:, j, c * BANK : (c + 1) * BANK],
-                    in_=banks_of[n, j][c][:],
+                    in_=bank_of[n, j, c][:],
                     func=EXP,
                     bias=shift_of[n, j][:, 0:1],
                     scale=SCORE_SCALE,
@@ -212,12 +217,12 @@ def tile_multiheadattention_pa_kernel(tc, qh, kh, vh, out):
                 [P, LQ, PACK], BF16, tag="grouped", name="grouped%d" % n, align_bytes=64
             )
 
-        def multiply_and_group(engine, n, factors, lo, hi):
-            runs = (hi - lo) // RUN
+        def multiply_and_group(engine, n, factors, lo, hi, run=RUN):
+            runs = (hi - lo) // run
             engine.tensor_tensor(
-                out=grouped_of[n][:, lo:hi, :].rearrange("p (c i) j -> p c j i", i=RUN),
-                in0=e_of[n][:, :, lo:hi].rearrange("p j (c i) -> p c j i", i=RUN),
-                in1=factors[:].unsqueeze(1).unsqueeze(3).to_broadcast([P, runs, PACK, RUN]),
+                out=grouped_of[n][:, lo:hi, :].rearrange("p (c i) j -> p c j i", i=run),
+                in0=e_of[n][:, :, lo:hi].rearrange("p j (c i) -> p c j i", i=run),
+                in1=factors[:].unsqueeze(1).unsqueeze(3).to_broadcast([P, runs, PACK, run]),
                 op=ALU.mult,
             )
 
@@ -225,7 +230,7 @@ def tile_multiheadattention_pa_kernel(tc, qh, kh, vh, out):
             multiply_and_group(nc.vector, n, spread_of[n], lo, hi)
 
         def group_by_gpsimd(n, lo, hi):
-            multiply_and_group(nc.gpsimd, n, recip_of[n], lo, hi)
+            multiply_and_group(nc.gpsimd, n, recip_of[n], lo, hi, 2 * RUN)
 
         def group_by_scalar(n, lo, hi):
             planes = plane_pool.tile([P, PACK, hi - lo], BF16, tag="planes%d" % (hi - lo), name="planes%d" % n)
@@ -278,14 +283,24 @@ def tile_multiheadattention_pa_kernel(tc, qh, kh, vh, out):
                 nc.scalar.copy(out=result[:], in_=acc[:])
             nc.sync.dma_start(out=rows[:, t0:t1, :], in_=result[:])
 
-        for part in range(4):
-            transpose_part(0, part)
+        transpose_part(0, 0)
+        transpose_part(0, 1)
+        transpose_part(0, 2)
+        scores(0, 0, 0)
+        scores(0, 0, 1)
+        transpose_part(0, 3)
         for h in range(HEADS):
             regroup_values(h)
 
         last = GROUPS - 1
         step = VECTOR_QUERIES // VECTOR_PARTS
-        scalar_end = VECTOR_QUERIES + SCALAR_QUERIES
+
+        def vector_end(n):
+            return FIRST_VECTOR if n == 0 else VECTOR_QUERIES
+
+        def scalar_end(n):
+            return vector_end(n) + (FIRST_SCALAR if n == 0 else SCALAR_QUERIES)
+
         for slot in range(GROUPS * PACK):
             n, j = divmod(slot, PACK)
 
@@ -293,7 +308,9 @@ def tile_multiheadattention_pa_kernel(tc, qh, kh, vh, out):
                 m, rest = divmod(slot - lag, PACK)
                 return m if rest == 0 and 0 <= m < last else None
 
-            scores(n, j)
+            if slot > 0:
+                for c in range(HALVES):
+                    scores(n, j, c)
             joined, ready = due(JOIN), due(JOIN + 4)
             maximum(n, j, 0)
             if 0 < slot <= EARLY:
@@ -307,23 +324,25 @@ def tile_multiheadattention_pa_kernel(tc, qh, kh, vh, out):
             for part in range(VECTOR_PARTS):
                 m = due(JOIN + 1 + part)
                 if m is not None:
+                    step = vector_end(m) // VECTOR_PARTS
                     group_by_vector(m, part * step, (part + 1) * step)
             if slot == JOIN:
-                shift(n, j)
-                quantise_values()
+                quantise_values(0, 2)
             if joined is not None:
                 invert(joined)
-            if slot >= EARLY and slot != JOIN:
+            if slot >= EARLY:
                 shift(n, j)
+            if slot == QV2:
+                quantise_values(2, HEADS)
             if ready is not None:
                 quantise(ready, 0, LQ)
             if joined is not None:
                 open_group(joined)
-                group_by_gpsimd(joined, scalar_end + (VECTOR_MORE if joined == last - 1 else 0), LQ)
+                group_by_gpsimd(joined, scalar_end(joined) + (VECTOR_MORE if joined == last - 1 else 0), LQ)
             if slot >= EARLY:
                 exponentials(n, j)
-            if joined is not None:
-                group_by_scalar(joined, VECTOR_QUERIES, scalar_end)
+            if joined is not None and scalar_end(joined) > vector_end(joined):
+                group_by_scalar(joined, vector_end(joined), scalar_end(joined))
             if n in TURN_GROUPS:
                 for part in TURNS[j]:
                     transpose_part(1 + TURN_GROUPS.index(n), part)
@@ -332,9 +351,12 @@ def tile_multiheadattention_pa_kernel(tc, qh, kh, vh, out):
                 if m is not None and m % PASSES == PASSES - 1 and n < last:
                     multiply(m // PASSES, b * PACK, (b + 1) * PACK, "scalar")
 
-        group_by_vector(last - 1, 2 * step, VECTOR_QUERIES)
-        group_by_vector(last - 1, scalar_end, scalar_end + VECTOR_MORE)
+        for part in range(7 - JOIN, VECTOR_PARTS):
+            group_by_vector(last - 1, part * step, (part + 1) * step)
+        more = scalar_end(last - 1)
+        group_by_vector(last - 1, more, more + VECTOR_MORE // 2)
         add_halves(last)
+        group_by_vector(last - 1, more + VECTOR_MORE // 2, more + VECTOR_MORE)
         invert(last)
         spread(last)
         quantise(last - 1, 0, LQ)

@@ -31,6 +31,7 @@ VECTOR_PARTS = 4
 VECTOR_MORE = 128
 LAST_VECTOR, LAST_GPSIMD = 512, 192
 EARLY = 3
+WARM_UP = 3
 FIRST_VECTOR, FIRST_SCALAR = 352, 0
 QV2 = 9
 TURN_GROUPS = (1, 2, 4)
@@ -87,6 +88,12 @@ def tile_multiheadattention_pa_kernel(tc, qh, kh, vh, out):
         make_identity(nc, ident[:])
         ident_f32 = const.tile([P, P], F32)
         make_identity(nc, ident_f32[:])
+
+        zeros = const.tile([P, BANK], BF16)
+        nc.vector.memset(zeros[:], 0.0)
+        busy = psum.tile([P, BANK], F32, tag="bank", name="busy")
+        for k in range(WARM_UP):
+            nc.tensor.matmul(busy[:], lhsT=zeros[:, :P], rhs=zeros[:], start=True, stop=True)
 
         warm_in = const.tile([P, 1], F32)
         warm_out = const.tile([P, 1], F32)
@@ -217,12 +224,12 @@ def tile_multiheadattention_pa_kernel(tc, qh, kh, vh, out):
                 [P, LQ, PACK], BF16, tag="grouped", name="grouped%d" % n, align_bytes=64
             )
 
-        def multiply_and_group(engine, n, factors, lo, hi, run=RUN):
-            runs = (hi - lo) // run
+        def multiply_and_group(engine, n, factors, lo, hi):
+            runs = (hi - lo) // RUN
             engine.tensor_tensor(
-                out=grouped_of[n][:, lo:hi, :].rearrange("p (c i) j -> p c j i", i=run),
-                in0=e_of[n][:, :, lo:hi].rearrange("p j (c i) -> p c j i", i=run),
-                in1=factors[:].unsqueeze(1).unsqueeze(3).to_broadcast([P, runs, PACK, run]),
+                out=grouped_of[n][:, lo:hi, :].rearrange("p (c i) j -> p c j i", i=RUN),
+                in0=e_of[n][:, :, lo:hi].rearrange("p j (c i) -> p c j i", i=RUN),
+                in1=factors[:].unsqueeze(1).unsqueeze(3).to_broadcast([P, runs, PACK, RUN]),
                 op=ALU.mult,
             )
 
@@ -230,7 +237,7 @@ def tile_multiheadattention_pa_kernel(tc, qh, kh, vh, out):
             multiply_and_group(nc.vector, n, spread_of[n], lo, hi)
 
         def group_by_gpsimd(n, lo, hi):
-            multiply_and_group(nc.gpsimd, n, recip_of[n], lo, hi, 2 * RUN)
+            multiply_and_group(nc.gpsimd, n, recip_of[n], lo, hi)
 
         def group_by_scalar(n, lo, hi):
             planes = plane_pool.tile([P, PACK, hi - lo], BF16, tag="planes%d" % (hi - lo), name="planes%d" % n)

@@ -26,12 +26,15 @@ HALVES = LQ // BANK
 SCORE_SCALE = 1.0 / math.sqrt(2048.0)
 RUN = 4
 
-VECTOR_QUERIES, SCALAR_QUERIES = 256, 144
+VECTOR_QUERIES, SCALAR_QUERIES = 272, 128
 VECTOR_PARTS = 4
 VECTOR_MORE = 128
 LAST_VECTOR, LAST_GPSIMD = 512, 192
 EARLY = 3
 WARM_UP = 3
+MX_LAGS = (10, 11)
+STORE_LAG = 0
+STOP = 28
 FIRST_VECTOR, FIRST_SCALAR = 352, 0
 QV2 = 9
 TURN_GROUPS = (1, 2, 4)
@@ -158,6 +161,7 @@ def tile_multiheadattention_pa_kernel(tc, qh, kh, vh, out):
         bank_of = {}
         half_max_of = {}
         shift_of = {}
+        acc_of = {}
 
         def scores(n, j, c):
             h, g = divmod(n, PASSES)
@@ -268,9 +272,9 @@ def tile_multiheadattention_pa_kernel(tc, qh, kh, vh, out):
                 in_=grouped_of[n][:, lo:hi, :].rearrange("p q j -> p (q j)"),
             )
 
-        def multiply(h, t0, t1, engine):
-            rows = out[h].rearrange("(p t) d -> p t d", t=Q_TILES)
+        def multiply(h, t0, t1):
             acc = psum.tile([P, t1 - t0, DV], F32, tag="bank", name="acc%d_%d" % (h, t0))
+            acc_of[h, t0] = acc
             for t in range(t0, t1):
                 cols = slice(t * P, (t + 1) * P)
                 for g in range(PASSES):
@@ -283,11 +287,14 @@ def tile_multiheadattention_pa_kernel(tc, qh, kh, vh, out):
                         start=(g == 0),
                         stop=(g == PASSES - 1),
                     )
+
+        def store(h, t0, t1, engine):
+            rows = out[h].rearrange("(p t) d -> p t d", t=Q_TILES)
             result = out_pool.tile([P, t1 - t0, DV], F32, tag="result", name="res%d_%d" % (h, t0))
             if engine == "vector":
-                nc.vector.tensor_copy(out=result[:], in_=acc[:])
+                nc.vector.tensor_copy(out=result[:], in_=acc_of[h, t0][:])
             else:
-                nc.scalar.copy(out=result[:], in_=acc[:])
+                nc.scalar.copy(out=result[:], in_=acc_of[h, t0][:])
             nc.sync.dma_start(out=rows[:, t0:t1, :], in_=result[:])
 
         transpose_part(0, 0)
@@ -315,9 +322,6 @@ def tile_multiheadattention_pa_kernel(tc, qh, kh, vh, out):
                 m, rest = divmod(slot - lag, PACK)
                 return m if rest == 0 and 0 <= m < last else None
 
-            if slot > 0:
-                for c in range(HALVES):
-                    scores(n, j, c)
             joined, ready = due(JOIN), due(JOIN + 4)
             maximum(n, j, 0)
             if 0 < slot <= EARLY:
@@ -350,13 +354,19 @@ def tile_multiheadattention_pa_kernel(tc, qh, kh, vh, out):
                 exponentials(n, j)
             if joined is not None and scalar_end(joined) > vector_end(joined):
                 group_by_scalar(joined, vector_end(joined), scalar_end(joined))
+            if slot + 1 < GROUPS * PACK:
+                for c in range(HALVES):
+                    scores(*divmod(slot + 1, PACK), c)
             if n in TURN_GROUPS:
                 for part in TURNS[j]:
                     transpose_part(1 + TURN_GROUPS.index(n), part)
-            for b, lag in ((0, JOIN + 5), (1, JOIN + 6)):
+            for b, lag in enumerate(MX_LAGS):
                 m = due(lag)
-                if m is not None and m % PASSES == PASSES - 1 and n < last:
-                    multiply(m // PASSES, b * PACK, (b + 1) * PACK, "scalar")
+                if m is not None and m % PASSES == PASSES - 1 and slot + STORE_LAG < STOP:
+                    multiply(m // PASSES, b * PACK, (b + 1) * PACK)
+                m = due(lag + STORE_LAG)
+                if m is not None and m % PASSES == PASSES - 1 and slot < STOP:
+                    store(m // PASSES, b * PACK, (b + 1) * PACK, "scalar")
 
         for part in range(7 - JOIN, VECTOR_PARTS):
             group_by_vector(last - 1, part * step, (part + 1) * step)
@@ -373,7 +383,10 @@ def tile_multiheadattention_pa_kernel(tc, qh, kh, vh, out):
         group_by_vector(last, 0, LAST_VECTOR // 2)
         group_by_vector(last, LAST_VECTOR // 2, LAST_VECTOR)
         for b in range(2):
-            multiply(HEADS - 2, b * PACK, (b + 1) * PACK, "scalar")
+            if (HEADS - 2, b * PACK) not in acc_of:
+                multiply(HEADS - 2, b * PACK, (b + 1) * PACK)
+                store(HEADS - 2, b * PACK, (b + 1) * PACK, "scalar")
         for t0, t1 in ((0, 2), (2, 4), (4, 6), (6, 7), (7, 8)):
             quantise(last, t0 * P, t1 * P)
-            multiply(HEADS - 1, t0, t1, "vector" if t0 == 7 else "scalar")
+            multiply(HEADS - 1, t0, t1)
+            store(HEADS - 1, t0, t1, "vector" if t0 == 7 else "scalar")

from contextlib import ExitStack
import math

import concourse.mybir as mybir
from concourse.masks import make_identity

BF16 = mybir.dt.bfloat16
F32 = mybir.dt.float32
U32 = mybir.dt.uint32
U8 = mybir.dt.uint8
FP8X4 = mybir.dt.float8_e4m3fn_x4
EXP = mybir.ActivationFunctionType.Exp
COPY = mybir.ActivationFunctionType.Copy
ALU = mybir.AluOpType
AXIS_X = mybir.AxisListType.X

P = 128
PACK = 4
K_PASS = P * PACK
HEADS, LQ, LK, DK, DV = 4, 1024, 1024, 128, 128
PASSES = LK // K_PASS
GROUPS = HEADS * PASSES
Q_TILES = LQ // P
BANK = 512
HALVES = LQ // BANK
SCORE_SCALE = 1.0 / math.sqrt(2048.0)
RUN = 4

VECTOR_QUERIES, SCALAR_QUERIES = 272, 128
VECTOR_PARTS = 4
VECTOR_MORE = 128
LAST_VECTOR, LAST_GPSIMD = 512, 192
EARLY = 3
WARM_UP = 3
MX_LAGS = (10, 11)
STORE_LAG = 0
STOP = 28
FIRST_VECTOR, FIRST_SCALAR = 352, 0
QV2 = 9
TURN_GROUPS = (1, 2, 4)
JOIN = 5
TURNS = ((0,), (1,), (2,), (3,))

FLOPS = 2 * HEADS * LQ * LK * (DK + DV)


def tile_multiheadattention_pa_kernel(tc, qh, kh, vh, out):
    nc = tc.nc
    with ExitStack() as ctx:
        const = ctx.enter_context(tc.tile_pool(name="const", bufs=1))
        turned = ctx.enter_context(tc.tile_pool(name="turned", bufs=2))
        stats = ctx.enter_context(tc.tile_pool(name="stats", bufs=6))
        e_pool = ctx.enter_context(tc.tile_pool(name="e_pool", bufs=3))
        plane_pool = ctx.enter_context(tc.tile_pool(name="plane_pool", bufs=3))
        grouped_pool = ctx.enter_context(tc.tile_pool(name="grouped_pool", bufs=1))
        mx_pool = ctx.enter_context(tc.tile_pool(name="mx_pool", bufs=2))
        out_pool = ctx.enter_context(tc.tile_pool(name="out_pool", bufs=8))
        psum = ctx.enter_context(tc.psum_pool(name="psum", bufs=7))
        ctx.enter_context(tc.manual_schedule())

        q_in = const.tile([P, HEADS, Q_TILES, DK], BF16)
        k_in = const.tile([P, HEADS, PASSES * PACK, DK], BF16)
        v_in = const.tile([P, HEADS * PASSES, PACK, DV], BF16)

        def load_keys(h, g):
            nc.sync.dma_start(
                out=k_in[:, h, g * PACK : (g + 1) * PACK, :],
                in_=kh[h, g * K_PASS : (g + 1) * K_PASS, :].rearrange("(p j) d -> p j d", j=PACK),
            )

        def load_queries(h, t0, t1):
            rows = qh[h].rearrange("(p t) d -> p t d", t=Q_TILES)
            nc.sync.dma_start(out=q_in[:, h, t0:t1], in_=rows[:, t0:t1, :])

        for h in range(HEADS):
            load_keys(h, 0)
            if h == 0:
                load_queries(h, 0, PACK)
                load_queries(h, PACK, Q_TILES)
            else:
                load_queries(h, 0, Q_TILES)
            load_keys(h, 1)
            if h == 0:
                for k in range(HEADS):
                    nc.sync.dma_start(
                        out=v_in[:, k * PASSES : (k + 1) * PASSES],
                        in_=vh[k].rearrange("(g p j) d -> p g j d", g=PASSES, j=PACK),
                    )

        ident = const.tile([P, P], BF16)
        make_identity(nc, ident[:])
        ident_f32 = const.tile([P, P], F32)
        make_identity(nc, ident_f32[:])

        zeros = const.tile([P, BANK], BF16)
        nc.vector.memset(zeros[:], 0.0)
        busy = psum.tile([P, BANK], F32, tag="bank", name="busy")
        for k in range(WARM_UP):
            nc.tensor.matmul(busy[:], lhsT=zeros[:, :P], rhs=zeros[:], start=True, stop=True)

        warm_in = const.tile([P, 1], F32)
        warm_out = const.tile([P, 1], F32)
        nc.vector.memset(warm_in[:], 0.0)
        nc.scalar.activation(out=warm_out[:], in_=warm_in[:], func=EXP)

        v_grouped = const.tile([P, HEADS * PASSES, DV, PACK], BF16, align_bytes=64)
        v_words = const.tile([P, HEADS * PASSES, DV], U32, align_bytes=64)
        v_scales = const.tile([P, HEADS * PASSES, DV], U8, align_bytes=64)

        def regroup_values(h):
            rows = slice(h * PASSES, (h + 1) * PASSES)
            nc.gpsimd.tensor_scalar(
                out=v_grouped[:, rows],
                in0=v_in[:, rows].rearrange("p g j d -> p g d j"),
                scalar1=1.0,
                scalar2=0.0,
                op0=ALU.mult,
                op1=ALU.add,
            )

        def quantise_values(h0, h1):
            rows = slice(h0 * PASSES, h1 * PASSES)
            nc.vector.quantize_mx(
                out=v_words[:, rows].rearrange("p g d -> p (g d)").bitcast(FP8X4),
                scales=v_scales[:, rows].rearrange("p g d -> p (g d)"),
                in_=v_grouped[:, rows].rearrange("p g d j -> p (g d j)"),
            )

        kT = {}
        qT = {}

        def transpose_part(h, part):
            if part == 0:
                kT[h] = turned.tile([P, PASSES * PACK * P], BF16, tag="kT", name="kT%d" % h)
                qT[h] = turned.tile([P, LQ], BF16, tag="qT", name="qT%d" % h)
            keys = part in (0, 3)
            source, target = (k_in, kT[h]) if keys else (q_in, qT[h])
            half = part // 2 if keys else part - 1
            bank = psum.tile([P, BANK], BF16, tag="bank", name="turn%d_%d" % (h, part))
            for i in range(PACK):
                nc.tensor.transpose(
                    bank[:, i * P : (i + 1) * P], source[:, h, half * PACK + i, :], ident[:]
                )
            lo, mid, hi = half * BANK, half * BANK + BANK // 2, (half + 1) * BANK
            if h == 0 and part == 1:
                nc.scalar.copy(out=target[:, lo:mid], in_=bank[:, : BANK // 2])
                nc.vector.tensor_copy(out=target[:, mid:hi], in_=bank[:, BANK // 2 :])
            elif h == 0 and part % 2 == 0:
                nc.vector.tensor_copy(out=target[:, lo:hi], in_=bank[:])
            else:
                nc.scalar.copy(out=target[:, lo:hi], in_=bank[:])

        e_of = {}
        sums_of = {}
        total_of = {}
        recip_of = {}
        spread_of = {}
        grouped_of = {}
        words_of = {}
        scales_of = {}
        bank_of = {}
        half_max_of = {}
        shift_of = {}
        acc_of = {}

        def scores(n, j, c):
            h, g = divmod(n, PASSES)
            tile_cols = slice((g * PACK + j) * P, (g * PACK + j + 1) * P)
            bank_of[n, j, c] = psum.tile([P, BANK], F32, tag="bank", name="s%d_%d_%d" % (n, j, c))
            nc.tensor.matmul(
                bank_of[n, j, c][:],
                lhsT=kT[h][:, tile_cols],
                rhs=qT[h][:, c * BANK : (c + 1) * BANK],
                start=True,
                stop=True,
            )

        def maximum(n, j, c):
            if c == 0:
                half_max_of[n, j] = stats.tile(
                    [P, HALVES], F32, tag="half_max", name="half_max%d_%d" % (n, j)
                )
            nc.vector.tensor_reduce(
                out=half_max_of[n, j][:, c : c + 1], in_=bank_of[n, j, c][:], axis=AXIS_X, op=ALU.max
            )

        def shift(n, j):
            shift_of[n, j] = stats.tile([P, 1], F32, tag="shift", name="shift%d_%d" % (n, j))
            nc.vector.tensor_scalar(
                out=shift_of[n, j][:],
                in0=half_max_of[n, j][:, 0:1],
                scalar1=half_max_of[n, j][:, 1:2],
                scalar2=-SCORE_SCALE,
                op0=ALU.max,
                op1=ALU.mult,
            )

        def exponentials(n, j):
            if j == 0:
                e_of[n] = e_pool.tile([P, PACK, LQ], F32, tag="e", name="e%d" % n)
                sums_of[n] = stats.tile([P, PACK, HALVES], F32, tag="sums", name="sums%d" % n)
            for c in range(HALVES):
                nc.scalar.activation(
                    out=e_of[n][:, j, c * BANK : (c + 1) * BANK],
                    in_=bank_of[n, j, c][:],
                    func=EXP,
                    bias=shift_of[n, j][:, 0:1],
                    scale=SCORE_SCALE,
                    accum_out=sums_of[n][:, j, c : c + 1],
                )

        def add_halves(n):
            total_of[n] = stats.tile([P, PACK], F32, tag="total", name="total%d" % n)
            nc.vector.tensor_reduce(out=total_of[n][:], in_=sums_of[n][:], axis=AXIS_X, op=ALU.add)

        def invert(n):
            recip_of[n] = stats.tile([P, PACK], F32, tag="recip", name="recip%d" % n)
            nc.vector.reciprocal(out=recip_of[n][:], in_=total_of[n][:])

        def spread(n):
            spread_of[n] = psum.tile([P, PACK], F32, tag="spread", name="spread%d" % n, bufs=1)
            nc.tensor.matmul(
                spread_of[n][:], lhsT=ident_f32[:], rhs=recip_of[n][:], start=True, stop=True
            )

        def open_group(n):
            grouped_of[n] = grouped_pool.tile(
                [P, LQ, PACK], BF16, tag="grouped", name="grouped%d" % n, align_bytes=64
            )

        def multiply_and_group(engine, n, factors, lo, hi):
            runs = (hi - lo) // RUN
            engine.tensor_tensor(
                out=grouped_of[n][:, lo:hi, :].rearrange("p (c i) j -> p c j i", i=RUN),
                in0=e_of[n][:, :, lo:hi].rearrange("p j (c i) -> p c j i", i=RUN),
                in1=factors[:].unsqueeze(1).unsqueeze(3).to_broadcast([P, runs, PACK, RUN]),
                op=ALU.mult,
            )

        def group_by_vector(n, lo, hi):
            multiply_and_group(nc.vector, n, spread_of[n], lo, hi)

        def group_by_gpsimd(n, lo, hi):
            multiply_and_group(nc.gpsimd, n, recip_of[n], lo, hi)

        def group_by_scalar(n, lo, hi):
            planes = plane_pool.tile([P, PACK, hi - lo], BF16, tag="planes%d" % (hi - lo), name="planes%d" % n)
            for j in range(PACK):
                nc.scalar.activation(
                    out=planes[:, j, :],
                    in_=e_of[n][:, j, lo:hi],
                    func=COPY,
                    scale=recip_of[n][:, j : j + 1],
                )
            nc.scalar.copy(
                out=grouped_of[n][:, lo:hi, :].rearrange("p (c i) j -> p c j i", i=RUN),
                in_=planes[:].rearrange("p j (c i) -> p c j i", i=RUN),
            )

        def quantise(n, lo, hi):
            h, g = divmod(n, PASSES)
            if g == 0 and lo == 0:
                words_of[h] = mx_pool.tile(
                    [P, PASSES, LQ], U32, tag="words", name="words%d" % h, align_bytes=64
                )
                scales_of[h] = mx_pool.tile(
                    [P, PASSES, LQ], U8, tag="scales", name="scales%d" % h, align_bytes=64
                )
            nc.vector.quantize_mx(
                out=words_of[h][:, g, lo:hi].bitcast(FP8X4),
                scales=scales_of[h][:, g, lo:hi],
                in_=grouped_of[n][:, lo:hi, :].rearrange("p q j -> p (q j)"),
            )

        def multiply(h, t0, t1):
            acc = psum.tile([P, t1 - t0, DV], F32, tag="bank", name="acc%d_%d" % (h, t0))
            acc_of[h, t0] = acc
            for t in range(t0, t1):
                cols = slice(t * P, (t + 1) * P)
                for g in range(PASSES):
                    nc.tensor.matmul_mx(
                        out=acc[:, t - t0, :],
                        lhsT=words_of[h][:, g, cols].bitcast(FP8X4),
                        lhsT_scale=scales_of[h][:, g, cols],
                        rhs=v_words[:, h * PASSES + g, :].bitcast(FP8X4),
                        rhs_scale=v_scales[:, h * PASSES + g, :],
                        start=(g == 0),
                        stop=(g == PASSES - 1),
                    )

        def store(h, t0, t1, engine):
            rows = out[h].rearrange("(p t) d -> p t d", t=Q_TILES)
            result = out_pool.tile([P, t1 - t0, DV], F32, tag="result", name="res%d_%d" % (h, t0))
            if engine == "vector":
                nc.vector.tensor_copy(out=result[:], in_=acc_of[h, t0][:])
            else:
                nc.scalar.copy(out=result[:], in_=acc_of[h, t0][:])
            nc.sync.dma_start(out=rows[:, t0:t1, :], in_=result[:])

        transpose_part(0, 0)
        transpose_part(0, 1)
        transpose_part(0, 2)
        scores(0, 0, 0)
        scores(0, 0, 1)
        transpose_part(0, 3)
        for h in range(HEADS):
            regroup_values(h)

        last = GROUPS - 1
        step = VECTOR_QUERIES // VECTOR_PARTS

        def vector_end(n):
            return FIRST_VECTOR if n == 0 else VECTOR_QUERIES

        def scalar_end(n):
            return vector_end(n) + (FIRST_SCALAR if n == 0 else SCALAR_QUERIES)

        for slot in range(GROUPS * PACK):
            n, j = divmod(slot, PACK)

            def due(lag):
                m, rest = divmod(slot - lag, PACK)
                return m if rest == 0 and 0 <= m < last else None

            joined, ready = due(JOIN), due(JOIN + 4)
            maximum(n, j, 0)
            if 0 < slot <= EARLY:
                shift(*divmod(slot - 1, PACK))
                exponentials(*divmod(slot - 1, PACK))
            if joined is not None:
                add_halves(joined)
            maximum(n, j, 1)
            if due(JOIN + 1) is not None:
                spread(due(JOIN + 1))
            for part in range(VECTOR_PARTS):
                m = due(JOIN + 1 + part)
                if m is not None:
                    step = vector_end(m) // VECTOR_PARTS
                    group_by_vector(m, part * step, (part + 1) * step)
            if slot == JOIN:
                quantise_values(0, 2)
            if joined is not None:
                invert(joined)
            if slot >= EARLY:
                shift(n, j)
            if slot == QV2:
                quantise_values(2, HEADS)
            if ready is not None:
                quantise(ready, 0, LQ)
            if joined is not None:
                open_group(joined)
                group_by_gpsimd(joined, scalar_end(joined) + (VECTOR_MORE if joined == last - 1 else 0), LQ)
            if slot >= EARLY:
                exponentials(n, j)
            if joined is not None and scalar_end(joined) > vector_end(joined):
                group_by_scalar(joined, vector_end(joined), scalar_end(joined))
            if slot + 1 < GROUPS * PACK:
                for c in range(HALVES):
                    scores(*divmod(slot + 1, PACK), c)
            if n in TURN_GROUPS:
                for part in TURNS[j]:
                    transpose_part(1 + TURN_GROUPS.index(n), part)
            for b, lag in enumerate(MX_LAGS):
                m = due(lag)
                if m is not None and m % PASSES == PASSES - 1 and slot + STORE_LAG < STOP:
                    multiply(m // PASSES, b * PACK, (b + 1) * PACK)
                m = due(lag + STORE_LAG)
                if m is not None and m % PASSES == PASSES - 1 and slot < STOP:
                    store(m // PASSES, b * PACK, (b + 1) * PACK, "scalar")

        for part in range(7 - JOIN, VECTOR_PARTS):
            group_by_vector(last - 1, part * step, (part + 1) * step)
        more = scalar_end(last - 1)
        group_by_vector(last - 1, more, more + VECTOR_MORE // 2)
        add_halves(last)
        group_by_vector(last - 1, more + VECTOR_MORE // 2, more + VECTOR_MORE)
        invert(last)
        spread(last)
        quantise(last - 1, 0, LQ)
        open_group(last)
        group_by_gpsimd(last, LAST_VECTOR, LAST_VECTOR + LAST_GPSIMD)
        group_by_scalar(last, LAST_VECTOR + LAST_GPSIMD, LQ)
        group_by_vector(last, 0, LAST_VECTOR // 2)
        group_by_vector(last, LAST_VECTOR // 2, LAST_VECTOR)
        for b in range(2):
            if (HEADS - 2, b * PACK) not in acc_of:
                multiply(HEADS - 2, b * PACK, (b + 1) * PACK)
                store(HEADS - 2, b * PACK, (b + 1) * PACK, "scalar")
        for t0, t1 in ((0, 2), (2, 4), (4, 6), (6, 7), (7, 8)):
            quantise(last, t0 * P, t1 * P)
            multiply(HEADS - 1, t0, t1)
            store(HEADS - 1, t0, t1, "vector" if t0 == 7 else "scalar")
